import numpy as np
import ml_dtypes


def mxq(x, axis, fmt="e4m3"):
    dtype, down = {"e4m3": (ml_dtypes.float8_e4m3fn, 7), "e5m2": (ml_dtypes.float8_e5m2, 14)}[fmt]
    v = np.moveaxis(np.asarray(x, np.float32).astype(ml_dtypes.bfloat16).astype(np.float64), axis, -1)
    blocks = v.reshape(v.shape[:-1] + (-1, 32))
    amax = np.abs(blocks).max(-1, keepdims=True)
    byte = np.maximum(np.where(amax > 0, np.frexp(amax)[1] - 1 + 127, 0) - down, 1)
    scale = np.exp2(byte - 127.0)
    codes = (blocks / scale).astype(np.float32).astype(dtype).astype(np.float64)
    return np.moveaxis((codes * scale).reshape(v.shape), -1, axis)


WIDE = False


def mx_kscale(k):
    if not WIDE:
        return np.ones(k)
    levels = np.array([10, -10, 5, -5, 0])
    a = np.random.permutation(np.resize(levels, k // 512 * 4)).reshape(k // 512, 4)
    idx = np.arange(k)
    return np.exp2(a[idx // 512, idx % 128 // 32])


BF16 = ml_dtypes.bfloat16


def bf(x):
    return np.asarray(x, np.float32).astype(BF16)


def f64(x):
    return np.asarray(x).astype(np.float64)


E2M1 = np.array([0.0, 0.5, 1.0, 1.5, 2.0, 3.0, 4.0, 6.0, -0.0, -0.5, -1.0, -1.5, -2.0, -3.0, -4.0, -6.0])


def pack_weight(w, fmt):
    k, n = w.shape
    w = f64(bf(w)).reshape(k // 32, 32, n)
    amax = np.abs(w).max(1)
    if fmt == "e4m3":
        byte = np.frexp(amax)[1] - 1 + 127 - 7
    else:
        mant, ex = np.frexp(amax / 6.0)
        byte = np.where(mant > 0.5, ex, ex - 1) + 127
    byte = np.clip(np.where(amax > 0, byte, 1), 1, 254)
    scaled = (w * np.exp2(127.0 - byte)[:, None, :]).reshape(k, n).astype(np.float32)
    by_word = np.ascontiguousarray(scaled.reshape(k // 512, 128, 4, n).transpose(0, 1, 3, 2))
    if fmt == "e4m3":
        words = by_word.astype(ml_dtypes.float8_e4m3fn).view(np.uint8)
    else:
        c = by_word.astype(ml_dtypes.float4_e2m1fn).view(np.uint8) & 0xF
        words = c[..., 0::2] | (c[..., 1::2] << 4)
    return np.ascontiguousarray(words), np.ascontiguousarray(byte.astype(np.uint8).reshape(k // 512, 16, n))


def unpack_weight(words, scales, fmt):
    g, p, n, _ = words.shape
    if fmt == "e4m3":
        vals = np.ascontiguousarray(words).view(ml_dtypes.float8_e4m3fn).astype(np.float64)
    else:
        nib = np.empty((g, p, n, 4), np.uint8)
        nib[..., 0::2] = words & 0xF
        nib[..., 1::2] = words >> 4
        vals = E2M1[nib]
    vals = vals * np.repeat(np.exp2(scales.astype(np.float64) - 127.0), 8, axis=1)[..., None]
    return vals.transpose(0, 1, 3, 2).reshape(g * 512, n)

def pack4(w):
    words, scales = pack_weight(w, "e2m1")
    return words.reshape(words.shape[0], 128, -1), scales


def unpack4(words, scales):
    return unpack_weight(words.reshape(words.shape[0], 128, -1, 2), scales, "e2m1")


B, C, T, H = 4, 1536, 512, 512
EPS_LN = 1e-5
EPS_STD = 1e-5


def ln_dim1(z, g, b):
    mu = z.mean(axis=1, keepdims=True)
    var = ((z - mu) ** 2).mean(axis=1, keepdims=True)
    return (z - mu) / np.sqrt(var + EPS_LN) * g[None, :, None] + b[None, :, None]


def stats(x, m):
    mean = (m * x).sum(axis=2)
    std = np.sqrt(np.maximum((m * x * x).sum(axis=2) - mean ** 2, EPS_STD))
    return mean, std


def setup_inputs():
    s = mx_kscale(H)
    drop = np.random.randint(B, size=T)
    mask = (np.arange(B)[:, None, None] != drop[None, None, :]) * 1.0
    off = 0.5 * np.random.standard_normal((B, C, 1))
    gain = 0.5 + np.random.random((B, C, 1))
    pad = np.random.standard_normal((B, C, 1)) * (1.0 - mask)
    x = off + gain * np.random.standard_normal((B, C, T)) + pad
    h = bf(np.tanh(np.random.standard_normal((B, H, T))) * s[None, :, None])
    w2 = np.random.standard_normal((C, H)) * 3.0 / np.sqrt(H) / s[None, :]
    w2_words, w2_scales = pack4(np.ascontiguousarray(w2.T))
    return {"h": h,
            "x": bf(x),
            "mask": bf(mask),
            "w2_words": w2_words,
            "w2_scales": w2_scales,
            "b2": bf(0.1 * np.random.standard_normal(C)),
            "g2": bf(1.0 + 0.1 * np.random.standard_normal(2 * C)),
            "be2": bf(0.1 * np.random.standard_normal(2 * C))}


def reference(h, x, mask, w2_words, w2_scales, b2, g2, be2):
    x, mask = f64(x), f64(mask)
    alpha = (unpack4(w2_words, w2_scales).T @ mxq(f64(h), 1, "e4m3")) + f64(b2)[None, :, None]
    alpha = np.where(mask == 0, -np.inf, alpha)
    e = np.exp(alpha - alpha.max(axis=2, keepdims=True))
    alpha = e / e.sum(axis=2, keepdims=True)
    mean, std = stats(x, alpha)
    out = np.concatenate([mean, std], axis=1)[:, :, None]
    return ln_dim1(out, f64(g2), f64(be2))

@@ -1,0 +1,281 @@
+from contextlib import ExitStack
+
+import concourse.mybir as mybir
+from concourse.masks import make_identity
+
+F32 = mybir.dt.float32
+BF16 = mybir.dt.bfloat16
+I32 = mybir.dt.int32
+U32 = mybir.dt.uint32
+U8 = mybir.dt.uint8
+FP8X4 = mybir.dt.float8_e4m3fn_x4
+FP4X4 = mybir.dt.float4_e2m1fn_x4
+ALU = mybir.AluOpType
+ACT = mybir.ActivationFunctionType
+AX = mybir.AxisListType
+
+B, C, T, H = 4, 1536, 512, 512
+EPS_LN = 1e-5
+EPS_STD = 1e-5
+P = 128
+PACK = 4
+C_TILES = C // P
+N_TILES = B * C_TILES
+X_GROUP = 4
+V_COLS = 2 * C_TILES
+HUGE = 3.0e38
+
+FLOPS = 2 * B * C * T * H
+
+
+def tile_attentivestatspool_pb_kernel(tc, h, x, mask, w2_words, w2_scales, b2, g2, be2, out):
+    nc = tc.nc
+    with ExitStack() as stack:
+        stack.enter_context(tc.manual_schedule())
+        keep = stack.enter_context(tc.tile_pool(name="keep", bufs=1))
+        work = stack.enter_context(tc.tile_pool(name="work", bufs=3))
+        banks = stack.enter_context(tc.psum_pool(name="banks", bufs=4))
+        small_banks = stack.enter_context(tc.psum_pool(name="small_banks", bufs=1))
+
+        h_raw = []
+        for b in range(B):
+            h_raw.append(keep.tile([P, PACK, T], BF16, name="h_raw_%d" % b))
+        x_sb = []
+        for i in range(N_TILES // X_GROUP):
+            x_sb.append(keep.tile([P, X_GROUP, T], BF16, name="x_sb_%d" % i))
+        w_words = keep.tile([P, 2 * C], U8, align_bytes=64)
+        w_planes = keep.tile([P, C], U8, align_bytes=64)
+        nc.vector.memset(w_planes[:].bitcast(I32), 0)
+
+        def load_h(b):
+            nc.sync.dma_start(out=h_raw[b][:], in_=h[b].rearrange("(p j) t -> p j t", j=PACK))
+
+        def load_x(i):
+            b, first = divmod(i * X_GROUP, C_TILES)
+            rows = x[b].rearrange("(ct p) t -> p ct t", p=P)
+            nc.sync.dma_start(out=x_sb[i][:], in_=rows[:, first : first + X_GROUP, :])
+
+        load_h(0)
+        nc.sync.dma_start(
+            out=w_words[:].bitcast(I32), in_=w2_words.rearrange("g p n -> (g p) n").bitcast(I32)
+        )
+        for quadrant in range(4):
+            nc.sync.dma_start(
+                out=w_planes[32 * quadrant : 32 * quadrant + 4, :].bitcast(I32),
+                in_=w2_scales[0, 4 * quadrant : 4 * quadrant + 4, :].bitcast(I32),
+            )
+        groups_per_b = C_TILES // X_GROUP
+        for b in range(B):
+            for g in range(groups_per_b):
+                load_x(b * groups_per_b + g)
+            if b + 1 < B:
+                load_h(b + 1)
+
+        mask_sb = keep.tile([P, B, T], BF16)
+        for b in range(B):
+            nc.scalar.dma_start(out=mask_sb[:, b, :], in_=mask[b, 0].partition_broadcast(P))
+        gain_rows = keep.tile([P, P], BF16)
+        nc.gpsimd.memset(gain_rows[:], 0.0)
+        nc.scalar.dma_start(out=gain_rows[0:V_COLS, :], in_=g2.rearrange("(j p) -> j p", p=P))
+        nc.scalar.dma_start(
+            out=gain_rows[V_COLS : 2 * V_COLS, :], in_=be2.rearrange("(j p) -> j p", p=P)
+        )
+
+        identity = keep.tile([P, P], F32)
+        make_identity(nc, identity[:])
+        ones = keep.tile([P, P], F32)
+        nc.gpsimd.memset(ones[:], 1.0)
+        result = keep.tile([P, P], F32)
+        nc.gpsimd.memset(result[:], 0.0)
+
+        gain_rows_f32 = keep.tile([P, P], F32)
+        nc.scalar.copy(out=gain_rows_f32[:], in_=gain_rows[:])
+        gain_bank = small_banks.tile([P, P], F32)
+        nc.tensor.transpose(gain_bank[:], gain_rows_f32[:], identity[:])
+        gain_bias = keep.tile([P, 2 * V_COLS], F32)
+        nc.scalar.copy(out=gain_bias[:], in_=gain_bank[:, 0 : 2 * V_COLS])
+
+        h_codes = keep.tile([P, B, T], U32, align_bytes=64)
+        h_planes = keep.tile([P, B, T], U8, align_bytes=64)
+        h_grouped = []
+        for b in range(B):
+            h_grouped.append(keep.tile([P, T, PACK], BF16, name="h_grouped_%d" % b, align_bytes=64))
+
+        def regroup_h(b):
+            nc.vector.tensor_copy(
+                out=h_grouped[b][:].rearrange("p (c i) j -> p c j i", i=4),
+                in_=h_raw[b][:].rearrange("p j (c i) -> p c j i", i=4),
+            )
+
+        def quantise_h(b):
+            nc.vector.quantize_mx(
+                out=h_codes[:, b, :].bitcast(FP8X4),
+                scales=h_planes[:, b, :],
+                in_=h_grouped[b][:].rearrange("p t j -> p (t j)"),
+            )
+
+        cap = keep.tile([P, B, T], F32)
+
+        def make_cap(b):
+            nc.vector.tensor_scalar(
+                out=cap[:, b, :], in0=mask_sb[:, b, :], scalar1=0.5, scalar2=HUGE,
+                op0=ALU.subtract, op1=ALU.mult,
+            )
+
+        make_cap(0)
+        regroup_h(0)
+        for b in range(1, B):
+            make_cap(b)
+        quantise_h(0)
+
+        neg_max = keep.tile([P, N_TILES], F32)
+        s0 = keep.tile([P, N_TILES], F32)
+        s1 = keep.tile([P, N_TILES], F32)
+        s2 = keep.tile([P, N_TILES], F32)
+        masked = {}
+        weight = {}
+        weighted = {}
+        weighted_sq = {}
+
+        def x_tile(i):
+            return x_sb[i // X_GROUP][:, i % X_GROUP, :]
+
+        def logits_and_mask(i):
+            b, ct = divmod(i, C_TILES)
+            logits = banks.tile([P, T], F32)
+            nc.tensor.matmul_mx(
+                out=logits[:],
+                lhsT=w_words[:, 2 * P * ct : 2 * P * (ct + 1)].bitcast(FP4X4),
+                lhsT_scale=w_planes[:, P * ct : P * (ct + 1)],
+                rhs=h_codes[:, b, :].bitcast(FP8X4),
+                rhs_scale=h_planes[:, b, :],
+                start=True,
+                stop=True,
+            )
+            am = work.tile([P, T], F32)
+            nc.vector.tensor_tensor(out=am[:], in0=logits[:], in1=cap[:, b, :], op=ALU.min)
+            masked[i] = am
+
+        def maximum(i):
+            nc.vector.tensor_reduce(
+                out=neg_max[:, i : i + 1], in_=masked[i][:], axis=AX.X, op=ALU.max, negate=True
+            )
+
+        def weights(i):
+            e = work.tile([P, T], F32)
+            nc.scalar.activation(
+                out=e[:], in_=masked[i][:], func=ACT.Exp, bias=neg_max[:, i : i + 1], scale=1.0,
+                accum_out=s0[:, i : i + 1],
+            )
+            weight[i] = e
+
+        def first_moment(i):
+            y = work.tile([P, T], F32)
+            nc.vector.scalar_tensor_tensor(
+                out=y[:], in0=weight[i][:], scalar=1.0, in1=x_tile(i), op0=ALU.mult, op1=ALU.mult,
+                accum_out=s1[:, i : i + 1],
+            )
+            weighted[i] = y
+
+        def second_moment_products(i):
+            y2 = work.tile([P, T], F32)
+            nc.gpsimd.tensor_tensor(out=y2[:], in0=weighted[i][:], in1=x_tile(i), op=ALU.mult)
+            weighted_sq[i] = y2
+
+        def second_moment_sum(i):
+            unused = work.tile([P, T], BF16)
+            nc.scalar.activation(
+                out=unused[:], in_=weighted_sq[i][:], func=ACT.Copy, accum_out=s2[:, i : i + 1]
+            )
+
+        def is_tile(i):
+            return 0 <= i < N_TILES
+
+        REGROUP_AT = 3
+        QUANTISE_AT = 7
+        for s in range(-1, N_TILES + 2):
+            if is_tile(s + 1):
+                logits_and_mask(s + 1)
+            if is_tile(s):
+                maximum(s)
+                weights(s)
+            if is_tile(s - 1):
+                first_moment(s - 1)
+                second_moment_products(s - 1)
+            if is_tile(s - 2):
+                second_moment_sum(s - 2)
+            b, ct = divmod(s, C_TILES)
+            if 0 <= b < B - 1 and ct == REGROUP_AT:
+                regroup_h(b + 1)
+            if 0 <= b < B - 1 and ct == QUANTISE_AT:
+                quantise_h(b + 1)
+
+        by_b = "p (b c) -> p b c"
+        inv_s0 = keep.tile([P, N_TILES], F32)
+        nc.vector.reciprocal(out=inv_s0[:], in_=s0[:])
+        pooled = keep.tile([P, B, 2, C_TILES], F32)
+        mean = pooled[:, :, 0, :]
+        nc.vector.tensor_tensor(
+            out=mean, in0=s1[:].rearrange(by_b, b=B), in1=inv_s0[:].rearrange(by_b, b=B), op=ALU.mult
+        )
+        second = keep.tile([P, B, C_TILES], F32)
+        nc.vector.tensor_tensor(
+            out=second[:], in0=s2[:].rearrange(by_b, b=B), in1=inv_s0[:].rearrange(by_b, b=B),
+            op=ALU.mult,
+        )
+        mean_sq = keep.tile([P, B, C_TILES], F32)
+        nc.vector.tensor_tensor(out=mean_sq[:], in0=mean, in1=mean, op=ALU.mult)
+        var = keep.tile([P, B, C_TILES], F32)
+        nc.vector.tensor_tensor(out=var[:], in0=second[:], in1=mean_sq[:], op=ALU.subtract)
+        var_floor = keep.tile([P, B, C_TILES], F32)
+        nc.vector.tensor_scalar_max(out=var_floor[:], in0=var[:], scalar1=EPS_STD)
+        nc.scalar.activation(out=pooled[:, :, 1, :], in_=var_floor[:], func=ACT.Sqrt)
+
+        sums = keep.tile([P, 2 * B], F32)
+        squares = keep.tile([P, B, C_TILES], F32)
+        nc.vector.tensor_tensor(out=squares[:], in0=mean_sq[:], in1=var_floor[:], op=ALU.add)
+        nc.vector.tensor_reduce(out=sums[:, B : 2 * B], in_=squares[:], axis=AX.X, op=ALU.add)
+        pooled_rows = pooled[:].rearrange("p b s c -> p b (s c)")
+        nc.vector.tensor_reduce(out=sums[:, 0:B], in_=pooled_rows, axis=AX.X, op=ALU.add)
+        totals = small_banks.tile([P, 2 * B], F32)
+        nc.tensor.matmul(out=totals[:], lhsT=ones[:], rhs=sums[:], start=True, stop=True)
+        moments = keep.tile([P, 2 * B], F32)
+        nc.vector.tensor_scalar_mul(out=moments[:], in0=totals[:], scalar1=1.0 / (2 * C))
+        mu = moments[:, 0:B]
+        wide = [P, B, V_COLS]
+        centred = keep.tile(wide, F32)
+        nc.vector.tensor_tensor(
+            out=centred[:], in0=pooled_rows, in1=mu.unsqueeze(2).to_broadcast(wide), op=ALU.subtract
+        )
+        mu_sq = keep.tile([P, B], F32)
+        nc.vector.tensor_tensor(out=mu_sq[:], in0=mu, in1=mu, op=ALU.mult)
+        ln_var = keep.tile([P, B], F32)
+        nc.vector.scalar_tensor_tensor(
+            out=ln_var[:], in0=moments[:, B : 2 * B], scalar=EPS_LN, in1=mu_sq[:],
+            op0=ALU.add, op1=ALU.subtract,
+        )
+        ln_std = keep.tile([P, B], F32)
+        nc.scalar.activation(out=ln_std[:], in_=ln_var[:], func=ACT.Sqrt)
+        gained = keep.tile(wide, F32)
+        nc.vector.tensor_tensor(
+            out=gained[:], in0=centred[:],
+            in1=gain_bias[:, 0:V_COLS].unsqueeze(1).to_broadcast(wide), op=ALU.mult,
+        )
+        inv_std = keep.tile([P, B], F32)
+        nc.vector.reciprocal(out=inv_std[:], in_=ln_std[:])
+        scaled = keep.tile(wide, F32)
+        nc.vector.tensor_tensor(
+            out=scaled[:], in0=gained[:], in1=inv_std[:].unsqueeze(2).to_broadcast(wide), op=ALU.mult
+        )
+        nc.vector.tensor_tensor(
+            out=result[:, 0 : B * V_COLS].rearrange("p (b j) -> p b j", b=B), in0=scaled[:],
+            in1=gain_bias[:, V_COLS : 2 * V_COLS].unsqueeze(1).to_broadcast(wide), op=ALU.add,
+        )
+
+        result_bank = small_banks.tile([P, P], F32)
+        nc.tensor.transpose(result_bank[:], result[:], identity[:])
+        out_rows = keep.tile([P, P], F32)
+        nc.vector.tensor_copy(out=out_rows[:], in_=result_bank[:])
+        nc.sync.dma_start(
+            out=out.rearrange("b (j p) o -> (b j) (p o)", p=P), in_=out_rows[0 : B * V_COLS, :]
+        )

@@ -23,7 +23,17 @@ C_TILES = C // P
 N_TILES = B * C_TILES
 X_GROUP = 4
 V_COLS = 2 * C_TILES
+C_CHUNK = 512
+T_TILES = T // P
 HUGE = 3.0e38
+
+MASK_AT = 2 * V_COLS
+TRANSPOSE_AHEAD = 2
+MASK_AHEAD = TRANSPOSE_AHEAD + T_TILES
+LOGITS_AHEAD = MASK_AHEAD + 1
+UNITS_ALIVE = MASK_AHEAD + T_TILES
+REGROUP_AT = 0
+QUANTISE_AT = 2
 
 FLOPS = 2 * B * C * T * H
 
@@ -34,7 +44,9 @@ def tile_attentivestatspool_pb_kernel(tc, h, x, mask, w2_words, w2_scales, b2, g
         stack.enter_context(tc.manual_schedule())
         keep = stack.enter_context(tc.tile_pool(name="keep", bufs=1))
         work = stack.enter_context(tc.tile_pool(name="work", bufs=3))
-        banks = stack.enter_context(tc.psum_pool(name="banks", bufs=4))
+        units = stack.enter_context(tc.tile_pool(name="units", bufs=UNITS_ALIVE))
+        unit_banks = stack.enter_context(tc.psum_pool(name="unit_banks", bufs=2))
+        tile_banks = stack.enter_context(tc.psum_pool(name="tile_banks", bufs=4))
         small_banks = stack.enter_context(tc.psum_pool(name="small_banks", bufs=1))
 
         h_raw = []
@@ -68,17 +80,18 @@ def tile_attentivestatspool_pb_kernel(tc, h, x, mask, w2_words, w2_scales, b2, g
         for b in range(B):
             for g in range(groups_per_b):
                 load_x(b * groups_per_b + g)
-            if b + 1 < B:
-                load_h(b + 1)
+                if g == 0 and b + 1 < B:
+                    load_h(b + 1)
 
-        mask_sb = keep.tile([P, B, T], BF16)
-        for b in range(B):
-            nc.scalar.dma_start(out=mask_sb[:, b, :], in_=mask[b, 0].partition_broadcast(P))
-        gain_rows = keep.tile([P, P], BF16)
-        nc.gpsimd.memset(gain_rows[:], 0.0)
-        nc.scalar.dma_start(out=gain_rows[0:V_COLS, :], in_=g2.rearrange("(j p) -> j p", p=P))
+        vector_rows = keep.tile([P, P], BF16)
+        nc.gpsimd.memset(vector_rows[:], 0.0)
         nc.scalar.dma_start(
-            out=gain_rows[V_COLS : 2 * V_COLS, :], in_=be2.rearrange("(j p) -> j p", p=P)
+            out=vector_rows[MASK_AT : MASK_AT + B * T_TILES, :],
+            in_=mask.rearrange("b o (tt p) -> (b o tt) p", p=P),
+        )
+        nc.scalar.dma_start(out=vector_rows[0:V_COLS, :], in_=g2.rearrange("(j p) -> j p", p=P))
+        nc.scalar.dma_start(
+            out=vector_rows[V_COLS : 2 * V_COLS, :], in_=be2.rearrange("(j p) -> j p", p=P)
         )
 
         identity = keep.tile([P, P], F32)
@@ -87,13 +100,6 @@ def tile_attentivestatspool_pb_kernel(tc, h, x, mask, w2_words, w2_scales, b2, g
         nc.gpsimd.memset(ones[:], 1.0)
         result = keep.tile([P, P], F32)
         nc.gpsimd.memset(result[:], 0.0)
-
-        gain_rows_f32 = keep.tile([P, P], F32)
-        nc.scalar.copy(out=gain_rows_f32[:], in_=gain_rows[:])
-        gain_bank = small_banks.tile([P, P], F32)
-        nc.tensor.transpose(gain_bank[:], gain_rows_f32[:], identity[:])
-        gain_bias = keep.tile([P, 2 * V_COLS], F32)
-        nc.scalar.copy(out=gain_bias[:], in_=gain_bank[:, 0 : 2 * V_COLS])
 
         h_codes = keep.tile([P, B, T], U32, align_bytes=64)
         h_planes = keep.tile([P, B, T], U8, align_bytes=64)
@@ -114,46 +120,71 @@ def tile_attentivestatspool_pb_kernel(tc, h, x, mask, w2_words, w2_scales, b2, g
                 in_=h_grouped[b][:].rearrange("p t j -> p (t j)"),
             )
 
-        cap = keep.tile([P, B, T], F32)
-
-        def make_cap(b):
-            nc.vector.tensor_scalar(
-                out=cap[:, b, :], in0=mask_sb[:, b, :], scalar1=0.5, scalar2=HUGE,
-                op0=ALU.subtract, op1=ALU.mult,
-            )
-
-        make_cap(0)
         regroup_h(0)
-        for b in range(1, B):
-            make_cap(b)
+
+        vector_rows_f32 = keep.tile([P, P], F32)
+        nc.scalar.copy(out=vector_rows_f32[:], in_=vector_rows[:])
+        vector_bank = small_banks.tile([P, P], F32, tag="small")
+        nc.tensor.transpose(vector_bank[:], vector_rows_f32[:], identity[:])
+        vectors = keep.tile([P, MASK_AT + B * T_TILES], F32)
+        nc.scalar.copy(out=vectors[:], in_=vector_bank[:, 0 : MASK_AT + B * T_TILES])
+        gain = vectors[:, 0:V_COLS]
+        bias = vectors[:, V_COLS : 2 * V_COLS]
+        mask_one = vectors[:, MASK_AT : MASK_AT + B * T_TILES]
+        mask_bias = keep.tile([P, B * T_TILES], F32)
+        nc.vector.tensor_scalar(
+            out=mask_bias[:], in0=mask_one, scalar1=1.0, scalar2=HUGE, op0=ALU.subtract, op1=ALU.mult
+        )
+
         quantise_h(0)
 
         neg_max = keep.tile([P, N_TILES], F32)
         s0 = keep.tile([P, N_TILES], F32)
         s1 = keep.tile([P, N_TILES], F32)
         s2 = keep.tile([P, N_TILES], F32)
+        unit_bank = {}
+        unit_sb = {}
         masked = {}
         weight = {}
         weighted = {}
-        weighted_sq = {}
 
         def x_tile(i):
             return x_sb[i // X_GROUP][:, i % X_GROUP, :]
 
-        def logits_and_mask(i):
-            b, ct = divmod(i, C_TILES)
-            logits = banks.tile([P, T], F32)
+        def unit_logits(u):
+            b, rest = divmod(u, C_TILES)
+            cc, tt = divmod(rest, T_TILES)
+            logits = unit_banks.tile([P, C_CHUNK], F32)
             nc.tensor.matmul_mx(
                 out=logits[:],
-                lhsT=w_words[:, 2 * P * ct : 2 * P * (ct + 1)].bitcast(FP4X4),
-                lhsT_scale=w_planes[:, P * ct : P * (ct + 1)],
-                rhs=h_codes[:, b, :].bitcast(FP8X4),
-                rhs_scale=h_planes[:, b, :],
+                lhsT=h_codes[:, b, P * tt : P * (tt + 1)].bitcast(FP8X4),
+                lhsT_scale=h_planes[:, b, P * tt : P * (tt + 1)],
+                rhs=w_words[:, 2 * C_CHUNK * cc : 2 * C_CHUNK * (cc + 1)].bitcast(FP4X4),
+                rhs_scale=w_planes[:, C_CHUNK * cc : C_CHUNK * (cc + 1)],
                 start=True,
                 stop=True,
             )
-            am = work.tile([P, T], F32)
-            nc.vector.tensor_tensor(out=am[:], in0=logits[:], in1=cap[:, b, :], op=ALU.min)
+            unit_bank[u] = logits
+
+        def unit_mask(u):
+            column = T_TILES * (u // C_TILES) + u % T_TILES
+            am_t = units.tile([P, C_CHUNK], F32)
+            nc.scalar.activation(
+                out=am_t[:], in_=unit_bank[u][:], func=ACT.Identity,
+                bias=mask_bias[:, column : column + 1], scale=mask_one[:, column : column + 1],
+            )
+            unit_sb[u] = am_t
+
+        def tile_transposes(i):
+            first_unit = T_TILES * (i // T_TILES)
+            cl = i % T_TILES
+            am = tile_banks.tile([P, T], F32)
+            for tt in range(T_TILES):
+                nc.tensor.transpose(
+                    am[:, P * tt : P * (tt + 1)],
+                    unit_sb[first_unit + tt][:, P * cl : P * (cl + 1)],
+                    identity[:],
+                )
             masked[i] = am
 
         def maximum(i):
@@ -177,33 +208,30 @@ def tile_attentivestatspool_pb_kernel(tc, h, x, mask, w2_words, w2_scales, b2, g
             )
             weighted[i] = y
 
-        def second_moment_products(i):
-            y2 = work.tile([P, T], F32)
-            nc.gpsimd.tensor_tensor(out=y2[:], in0=weighted[i][:], in1=x_tile(i), op=ALU.mult)
-            weighted_sq[i] = y2
-
-        def second_moment_sum(i):
+        def second_moment(i):
             unused = work.tile([P, T], BF16)
-            nc.scalar.activation(
-                out=unused[:], in_=weighted_sq[i][:], func=ACT.Copy, accum_out=s2[:, i : i + 1]
+            nc.vector.scalar_tensor_tensor(
+                out=unused[:], in0=weighted[i][:], scalar=1.0, in1=x_tile(i), op0=ALU.mult,
+                op1=ALU.mult, accum_out=s2[:, i : i + 1],
             )
 
         def is_tile(i):
             return 0 <= i < N_TILES
 
-        REGROUP_AT = 3
-        QUANTISE_AT = 7
-        for s in range(-1, N_TILES + 2):
+        for s in range(-LOGITS_AHEAD, N_TILES + 2):
+            if is_tile(s + LOGITS_AHEAD):
+                unit_logits(s + LOGITS_AHEAD)
+            if is_tile(s + MASK_AHEAD):
+                unit_mask(s + MASK_AHEAD)
+            if is_tile(s + TRANSPOSE_AHEAD):
+                tile_transposes(s + TRANSPOSE_AHEAD)
             if is_tile(s + 1):
-                logits_and_mask(s + 1)
+                maximum(s + 1)
+                weights(s + 1)
             if is_tile(s):
-                maximum(s)
-                weights(s)
+                first_moment(s)
             if is_tile(s - 1):
-                first_moment(s - 1)
-                second_moment_products(s - 1)
-            if is_tile(s - 2):
-                second_moment_sum(s - 2)
+                second_moment(s - 1)
             b, ct = divmod(s, C_TILES)
             if 0 <= b < B - 1 and ct == REGROUP_AT:
                 regroup_h(b + 1)
@@ -237,7 +265,7 @@ def tile_attentivestatspool_pb_kernel(tc, h, x, mask, w2_words, w2_scales, b2, g
         nc.vector.tensor_reduce(out=sums[:, B : 2 * B], in_=squares[:], axis=AX.X, op=ALU.add)
         pooled_rows = pooled[:].rearrange("p b s c -> p b (s c)")
         nc.vector.tensor_reduce(out=sums[:, 0:B], in_=pooled_rows, axis=AX.X, op=ALU.add)
-        totals = small_banks.tile([P, 2 * B], F32)
+        totals = small_banks.tile([P, 2 * B], F32, tag="small")
         nc.tensor.matmul(out=totals[:], lhsT=ones[:], rhs=sums[:], start=True, stop=True)
         moments = keep.tile([P, 2 * B], F32)
         nc.vector.tensor_scalar_mul(out=moments[:], in0=totals[:], scalar1=1.0 / (2 * C))
@@ -259,7 +287,7 @@ def tile_attentivestatspool_pb_kernel(tc, h, x, mask, w2_words, w2_scales, b2, g
         gained = keep.tile(wide, F32)
         nc.vector.tensor_tensor(
             out=gained[:], in0=centred[:],
-            in1=gain_bias[:, 0:V_COLS].unsqueeze(1).to_broadcast(wide), op=ALU.mult,
+            in1=gain.unsqueeze(1).to_broadcast(wide), op=ALU.mult,
         )
         inv_std = keep.tile([P, B], F32)
         nc.vector.reciprocal(out=inv_std[:], in_=ln_std[:])
@@ -269,10 +297,10 @@ def tile_attentivestatspool_pb_kernel(tc, h, x, mask, w2_words, w2_scales, b2, g
         )
         nc.vector.tensor_tensor(
             out=result[:, 0 : B * V_COLS].rearrange("p (b j) -> p b j", b=B), in0=scaled[:],
-            in1=gain_bias[:, V_COLS : 2 * V_COLS].unsqueeze(1).to_broadcast(wide), op=ALU.add,
+            in1=bias.unsqueeze(1).to_broadcast(wide), op=ALU.add,
         )
 
-        result_bank = small_banks.tile([P, P], F32)
+        result_bank = small_banks.tile([P, P], F32, tag="small")
         nc.tensor.transpose(result_bank[:], result[:], identity[:])
         out_rows = keep.tile([P, P], F32)
         nc.vector.tensor_copy(out=out_rows[:], in_=result_bank[:])

@@ -28,12 +28,7 @@ T_TILES = T // P
 HUGE = 3.0e38
 
 MASK_AT = 2 * V_COLS
-TRANSPOSE_AHEAD = 2
-MASK_AHEAD = TRANSPOSE_AHEAD + T_TILES
-LOGITS_AHEAD = MASK_AHEAD + 1
-UNITS_ALIVE = MASK_AHEAD + T_TILES
-REGROUP_AT = 0
-QUANTISE_AT = 2
+N_CHUNKS = N_TILES // T_TILES
 
 FLOPS = 2 * B * C * T * H
 
@@ -43,11 +38,11 @@ def tile_attentivestatspool_pb_kernel(tc, h, x, mask, w2_words, w2_scales, b2, g
     with ExitStack() as stack:
         stack.enter_context(tc.manual_schedule())
         keep = stack.enter_context(tc.tile_pool(name="keep", bufs=1))
-        work = stack.enter_context(tc.tile_pool(name="work", bufs=3))
-        units = stack.enter_context(tc.tile_pool(name="units", bufs=UNITS_ALIVE))
-        unit_banks = stack.enter_context(tc.psum_pool(name="unit_banks", bufs=2))
-        tile_banks = stack.enter_context(tc.psum_pool(name="tile_banks", bufs=4))
-        small_banks = stack.enter_context(tc.psum_pool(name="small_banks", bufs=1))
+        units = stack.enter_context(tc.tile_pool(name="units", bufs=2 * T_TILES))
+        work = stack.enter_context(tc.tile_pool(name="work", bufs=2 * T_TILES))
+        scratch = stack.enter_context(tc.tile_pool(name="scratch", bufs=2))
+        unit_banks = stack.enter_context(tc.psum_pool(name="unit_banks", bufs=T_TILES))
+        tile_banks = stack.enter_context(tc.psum_pool(name="tile_banks", bufs=T_TILES))
 
         h_raw = []
         for b in range(B):
@@ -76,12 +71,10 @@ def tile_attentivestatspool_pb_kernel(tc, h, x, mask, w2_words, w2_scales, b2, g
                 out=w_planes[32 * quadrant : 32 * quadrant + 4, :].bitcast(I32),
                 in_=w2_scales[0, 4 * quadrant : 4 * quadrant + 4, :].bitcast(I32),
             )
-        groups_per_b = C_TILES // X_GROUP
-        for b in range(B):
-            for g in range(groups_per_b):
-                load_x(b * groups_per_b + g)
-                if g == 0 and b + 1 < B:
-                    load_h(b + 1)
+        for b in range(1, B):
+            load_h(b)
+        for i in range(N_TILES // X_GROUP):
+            load_x(i)
 
         vector_rows = keep.tile([P, P], BF16)
         nc.gpsimd.memset(vector_rows[:], 0.0)
@@ -124,7 +117,7 @@ def tile_attentivestatspool_pb_kernel(tc, h, x, mask, w2_words, w2_scales, b2, g
 
         vector_rows_f32 = keep.tile([P, P], F32)
         nc.scalar.copy(out=vector_rows_f32[:], in_=vector_rows[:])
-        vector_bank = small_banks.tile([P, P], F32, tag="small")
+        vector_bank = unit_banks.tile([P, P], F32, tag="logits")
         nc.tensor.transpose(vector_bank[:], vector_rows_f32[:], identity[:])
         vectors = keep.tile([P, MASK_AT + B * T_TILES], F32)
         nc.scalar.copy(out=vectors[:], in_=vector_bank[:, 0 : MASK_AT + B * T_TILES])
@@ -137,16 +130,23 @@ def tile_attentivestatspool_pb_kernel(tc, h, x, mask, w2_words, w2_scales, b2, g
         )
 
         quantise_h(0)
+        regroup_h(1)
+        for b in range(2, B):
+            regroup_h(b)
+            quantise_h(b - 1)
+        quantise_h(B - 1)
 
         neg_max = keep.tile([P, N_TILES], F32)
         s0 = keep.tile([P, N_TILES], F32)
         s1 = keep.tile([P, N_TILES], F32)
         s2 = keep.tile([P, N_TILES], F32)
+        s2_scalar = keep.tile([P, N_CHUNKS], F32)
         unit_bank = {}
         unit_sb = {}
         masked = {}
         weight = {}
         weighted = {}
+        weighted_sq = {}
 
         def x_tile(i):
             return x_sb[i // X_GROUP][:, i % X_GROUP, :]
@@ -209,34 +209,58 @@ def tile_attentivestatspool_pb_kernel(tc, h, x, mask, w2_words, w2_scales, b2, g
             weighted[i] = y
 
         def second_moment(i):
-            unused = work.tile([P, T], BF16)
+            unused = scratch.tile([P, T], BF16)
             nc.vector.scalar_tensor_tensor(
                 out=unused[:], in0=weighted[i][:], scalar=1.0, in1=x_tile(i), op0=ALU.mult,
                 op1=ALU.mult, accum_out=s2[:, i : i + 1],
             )
 
-        def is_tile(i):
-            return 0 <= i < N_TILES
+        def second_moment_products(i):
+            y2 = scratch.tile([P, T], F32)
+            nc.gpsimd.tensor_tensor(out=y2[:], in0=weighted[i][:], in1=x_tile(i), op=ALU.mult)
+            weighted_sq[i] = y2
 
-        for s in range(-LOGITS_AHEAD, N_TILES + 2):
-            if is_tile(s + LOGITS_AHEAD):
-                unit_logits(s + LOGITS_AHEAD)
-            if is_tile(s + MASK_AHEAD):
-                unit_mask(s + MASK_AHEAD)
-            if is_tile(s + TRANSPOSE_AHEAD):
-                tile_transposes(s + TRANSPOSE_AHEAD)
-            if is_tile(s + 1):
-                maximum(s + 1)
-                weights(s + 1)
-            if is_tile(s):
-                first_moment(s)
-            if is_tile(s - 1):
-                second_moment(s - 1)
-            b, ct = divmod(s, C_TILES)
-            if 0 <= b < B - 1 and ct == REGROUP_AT:
-                regroup_h(b + 1)
-            if 0 <= b < B - 1 and ct == QUANTISE_AT:
-                quantise_h(b + 1)
+        def second_moment_sum(i):
+            unused_sum = scratch.tile([P, T], BF16)
+            nc.scalar.activation(
+                out=unused_sum[:], in_=weighted_sq[i][:], func=ACT.Copy,
+                accum_out=s2_scalar[:, i // T_TILES : i // T_TILES + 1],
+            )
+
+        def members(n):
+            if 0 <= n < N_CHUNKS:
+                return list(range(T_TILES * n, T_TILES * (n + 1)))
+            return []
+
+        for r in range(-3, N_CHUNKS + 1):
+            for u in members(r + 3):
+                unit_logits(u)
+            for i in members(r + 2):
+                tile_transposes(i)
+            for i in members(r + 1):
+                maximum(i)
+            for i in members(r + 1):
+                weights(i)
+            for i in members(r - 1)[-1:]:
+                if i in weighted_sq:
+                    second_moment_sum(i)
+            for u in members(r + 3):
+                unit_mask(u)
+            for i in members(r)[:-1]:
+                first_moment(i)
+            for i in members(r)[:-1]:
+                second_moment(i)
+            for i in members(r)[-1:]:
+                first_moment(i)
+                if r < N_CHUNKS - 1:
+                    second_moment_products(i)
+                else:
+                    second_moment(i)
+
+        nc.vector.tensor_copy(
+            out=s2[:].rearrange("p (n cl) -> p n cl", cl=T_TILES)[:, 0 : N_CHUNKS - 1, T_TILES - 1],
+            in_=s2_scalar[:, 0 : N_CHUNKS - 1],
+        )
 
         by_b = "p (b c) -> p b c"
         inv_s0 = keep.tile([P, N_TILES], F32)
@@ -265,7 +289,7 @@ def tile_attentivestatspool_pb_kernel(tc, h, x, mask, w2_words, w2_scales, b2, g
         nc.vector.tensor_reduce(out=sums[:, B : 2 * B], in_=squares[:], axis=AX.X, op=ALU.add)
         pooled_rows = pooled[:].rearrange("p b s c -> p b (s c)")
         nc.vector.tensor_reduce(out=sums[:, 0:B], in_=pooled_rows, axis=AX.X, op=ALU.add)
-        totals = small_banks.tile([P, 2 * B], F32, tag="small")
+        totals = unit_banks.tile([P, 2 * B], F32, tag="logits")
         nc.tensor.matmul(out=totals[:], lhsT=ones[:], rhs=sums[:], start=True, stop=True)
         moments = keep.tile([P, 2 * B], F32)
         nc.vector.tensor_scalar_mul(out=moments[:], in0=totals[:], scalar1=1.0 / (2 * C))
@@ -300,7 +324,7 @@ def tile_attentivestatspool_pb_kernel(tc, h, x, mask, w2_words, w2_scales, b2, g
             in1=bias.unsqueeze(1).to_broadcast(wide), op=ALU.add,
         )
 
-        result_bank = small_banks.tile([P, P], F32, tag="small")
+        result_bank = unit_banks.tile([P, P], F32, tag="logits")
         nc.tensor.transpose(result_bank[:], result[:], identity[:])
         out_rows = keep.tile([P, P], F32)
         nc.vector.tensor_copy(out=out_rows[:], in_=result_bank[:])

@@ -29,6 +29,7 @@ HUGE = 3.0e38
 
 MASK_AT = 2 * V_COLS
 N_CHUNKS = N_TILES // T_TILES
+GPSIMD_TILES = 2
 
 FLOPS = 2 * B * C * T * H
 
@@ -40,7 +41,7 @@ def tile_attentivestatspool_pb_kernel(tc, h, x, mask, w2_words, w2_scales, b2, g
         keep = stack.enter_context(tc.tile_pool(name="keep", bufs=1))
         units = stack.enter_context(tc.tile_pool(name="units", bufs=2 * T_TILES))
         work = stack.enter_context(tc.tile_pool(name="work", bufs=2 * T_TILES))
-        scratch = stack.enter_context(tc.tile_pool(name="scratch", bufs=2))
+        scratch = stack.enter_context(tc.tile_pool(name="scratch", bufs=2 * GPSIMD_TILES))
         unit_banks = stack.enter_context(tc.psum_pool(name="unit_banks", bufs=T_TILES))
         tile_banks = stack.enter_context(tc.psum_pool(name="tile_banks", bufs=T_TILES))
 
@@ -140,7 +141,7 @@ def tile_attentivestatspool_pb_kernel(tc, h, x, mask, w2_words, w2_scales, b2, g
         s0 = keep.tile([P, N_TILES], F32)
         s1 = keep.tile([P, N_TILES], F32)
         s2 = keep.tile([P, N_TILES], F32)
-        s2_scalar = keep.tile([P, N_CHUNKS], F32)
+        s2_scalar = keep.tile([P, N_TILES], F32)
         unit_bank = {}
         unit_sb = {}
         masked = {}
@@ -224,7 +225,7 @@ def tile_attentivestatspool_pb_kernel(tc, h, x, mask, w2_words, w2_scales, b2, g
             unused_sum = scratch.tile([P, T], BF16)
             nc.scalar.activation(
                 out=unused_sum[:], in_=weighted_sq[i][:], func=ACT.Copy,
-                accum_out=s2_scalar[:, i // T_TILES : i // T_TILES + 1],
+                accum_out=s2_scalar[:, i : i + 1],
             )
 
         def members(n):
@@ -241,27 +242,25 @@ def tile_attentivestatspool_pb_kernel(tc, h, x, mask, w2_words, w2_scales, b2, g
                 maximum(i)
             for i in members(r + 1):
                 weights(i)
-            for i in members(r - 1)[-1:]:
+            for i in members(r - 1)[-GPSIMD_TILES:]:
                 if i in weighted_sq:
                     second_moment_sum(i)
             for u in members(r + 3):
                 unit_mask(u)
-            for i in members(r)[:-1]:
+            for i in members(r)[:-GPSIMD_TILES]:
                 first_moment(i)
-            for i in members(r)[:-1]:
+            for i in members(r)[:-GPSIMD_TILES]:
                 second_moment(i)
-            for i in members(r)[-1:]:
+            for i in members(r)[-GPSIMD_TILES:]:
                 first_moment(i)
                 if r < N_CHUNKS - 1:
                     second_moment_products(i)
-                else:
-                    second_moment(i)
 
+        by_chunk = "p (n cl) -> p n cl"
         nc.vector.tensor_copy(
-            out=s2[:].rearrange("p (n cl) -> p n cl", cl=T_TILES)[:, 0 : N_CHUNKS - 1, T_TILES - 1],
-            in_=s2_scalar[:, 0 : N_CHUNKS - 1],
+            out=s2[:].rearrange(by_chunk, cl=T_TILES)[:, 0 : N_CHUNKS - 1, T_TILES - GPSIMD_TILES :],
+            in_=s2_scalar[:].rearrange(by_chunk, cl=T_TILES)[:, 0 : N_CHUNKS - 1, T_TILES - GPSIMD_TILES :],
         )
-
         by_b = "p (b c) -> p b c"
         inv_s0 = keep.tile([P, N_TILES], F32)
         nc.vector.reciprocal(out=inv_s0[:], in_=s0[:])
@@ -270,13 +269,15 @@ def tile_attentivestatspool_pb_kernel(tc, h, x, mask, w2_words, w2_scales, b2, g
         nc.vector.tensor_tensor(
             out=mean, in0=s1[:].rearrange(by_b, b=B), in1=inv_s0[:].rearrange(by_b, b=B), op=ALU.mult
         )
+        for i in members(N_CHUNKS - 1)[-GPSIMD_TILES:]:
+            second_moment(i)
+        mean_sq = keep.tile([P, B, C_TILES], F32)
+        nc.vector.tensor_tensor(out=mean_sq[:], in0=mean, in1=mean, op=ALU.mult)
         second = keep.tile([P, B, C_TILES], F32)
         nc.vector.tensor_tensor(
             out=second[:], in0=s2[:].rearrange(by_b, b=B), in1=inv_s0[:].rearrange(by_b, b=B),
             op=ALU.mult,
         )
-        mean_sq = keep.tile([P, B, C_TILES], F32)
-        nc.vector.tensor_tensor(out=mean_sq[:], in0=mean, in1=mean, op=ALU.mult)
         var = keep.tile([P, B, C_TILES], F32)
         nc.vector.tensor_tensor(out=var[:], in0=second[:], in1=mean_sq[:], op=ALU.subtract)
         var_floor = keep.tile([P, B, C_TILES], F32)
@@ -328,6 +329,6 @@ def tile_attentivestatspool_pb_kernel(tc, h, x, mask, w2_words, w2_scales, b2, g
         nc.tensor.transpose(result_bank[:], result[:], identity[:])
         out_rows = keep.tile([P, P], F32)
         nc.vector.tensor_copy(out=out_rows[:], in_=result_bank[:])
-        nc.sync.dma_start(
-            out=out.rearrange("b (j p) o -> (b j) (p o)", p=P), in_=out_rows[0 : B * V_COLS, :]
-        )
+        out_view = out.rearrange("b (j p) o -> (b j) (p o)", p=P)
+        nc.sync.dma_start(out=out_view[0:64, :], in_=out_rows[0:64, :])
+        nc.sync.dma_start(out=out_view[64 : B * V_COLS, :], in_=out_rows[64 : B * V_COLS, :])

@@ -233,6 +233,14 @@ def tile_attentivestatspool_pb_kernel(tc, h, x, mask, w2_words, w2_scales, b2, g
                 return list(range(T_TILES * n, T_TILES * (n + 1)))
             return []
 
+        def gpsimd_share(n):
+            if n + 2 < N_CHUNKS:
+                return members(n)[T_TILES - GPSIMD_TILES :]
+            return []
+
+        def vector_share(n):
+            return members(n)[: T_TILES - len(gpsimd_share(n))]
+
         for r in range(-3, N_CHUNKS + 1):
             for u in members(r + 3):
                 unit_logits(u)
@@ -242,24 +250,22 @@ def tile_attentivestatspool_pb_kernel(tc, h, x, mask, w2_words, w2_scales, b2, g
                 maximum(i)
             for i in members(r + 1):
                 weights(i)
-            for i in members(r - 1)[-GPSIMD_TILES:]:
-                if i in weighted_sq:
-                    second_moment_sum(i)
+            for i in gpsimd_share(r - 1):
+                second_moment_sum(i)
             for u in members(r + 3):
                 unit_mask(u)
-            for i in members(r)[:-GPSIMD_TILES]:
+            for i in vector_share(r):
                 first_moment(i)
-            for i in members(r)[:-GPSIMD_TILES]:
+            for i in vector_share(r):
                 second_moment(i)
-            for i in members(r)[-GPSIMD_TILES:]:
+            for i in gpsimd_share(r):
                 first_moment(i)
-                if r < N_CHUNKS - 1:
-                    second_moment_products(i)
+                second_moment_products(i)
 
         by_chunk = "p (n cl) -> p n cl"
         nc.vector.tensor_copy(
-            out=s2[:].rearrange(by_chunk, cl=T_TILES)[:, 0 : N_CHUNKS - 1, T_TILES - GPSIMD_TILES :],
-            in_=s2_scalar[:].rearrange(by_chunk, cl=T_TILES)[:, 0 : N_CHUNKS - 1, T_TILES - GPSIMD_TILES :],
+            out=s2[:].rearrange(by_chunk, cl=T_TILES)[:, 0 : N_CHUNKS - 2, T_TILES - GPSIMD_TILES :],
+            in_=s2_scalar[:].rearrange(by_chunk, cl=T_TILES)[:, 0 : N_CHUNKS - 2, T_TILES - GPSIMD_TILES :],
         )
         by_b = "p (b c) -> p b c"
         inv_s0 = keep.tile([P, N_TILES], F32)
@@ -269,8 +275,6 @@ def tile_attentivestatspool_pb_kernel(tc, h, x, mask, w2_words, w2_scales, b2, g
         nc.vector.tensor_tensor(
             out=mean, in0=s1[:].rearrange(by_b, b=B), in1=inv_s0[:].rearrange(by_b, b=B), op=ALU.mult
         )
-        for i in members(N_CHUNKS - 1)[-GPSIMD_TILES:]:
-            second_moment(i)
         mean_sq = keep.tile([P, B, C_TILES], F32)
         nc.vector.tensor_tensor(out=mean_sq[:], in0=mean, in1=mean, op=ALU.mult)
         second = keep.tile([P, B, C_TILES], F32)

@@ -19,17 +19,21 @@ EPS_LN = 1e-5
 EPS_STD = 1e-5
 P = 128
 PACK = 4
+QUADRANT = 32
 C_TILES = C // P
 N_TILES = B * C_TILES
-X_GROUP = 4
-V_COLS = 2 * C_TILES
 C_CHUNK = 512
-T_TILES = T // P
-HUGE = 3.0e38
-
+PER_CHUNK = T // P
+N_CHUNKS = N_TILES // PER_CHUNK
+X_GROUP = PER_CHUNK
+V_COLS = 2 * C_TILES
 MASK_AT = 2 * V_COLS
-N_CHUNKS = N_TILES // T_TILES
+MASK_COLS = B * PER_CHUNK
+HUGE = 3.0e38
 GPSIMD_TILES = 2
+UNITS_AHEAD = 2
+TILES_AHEAD = 1
+STORE_SPLIT = 64
 
 FLOPS = 2 * B * C * T * H
 
@@ -39,11 +43,11 @@ def tile_attentivestatspool_pb_kernel(tc, h, x, mask, w2_words, w2_scales, b2, g
     with ExitStack() as stack:
         stack.enter_context(tc.manual_schedule())
         keep = stack.enter_context(tc.tile_pool(name="keep", bufs=1))
-        units = stack.enter_context(tc.tile_pool(name="units", bufs=2 * T_TILES))
-        work = stack.enter_context(tc.tile_pool(name="work", bufs=2 * T_TILES))
+        units = stack.enter_context(tc.tile_pool(name="units", bufs=2 * PER_CHUNK))
+        work = stack.enter_context(tc.tile_pool(name="work", bufs=2 * PER_CHUNK))
         scratch = stack.enter_context(tc.tile_pool(name="scratch", bufs=2 * GPSIMD_TILES))
-        unit_banks = stack.enter_context(tc.psum_pool(name="unit_banks", bufs=T_TILES))
-        tile_banks = stack.enter_context(tc.psum_pool(name="tile_banks", bufs=T_TILES))
+        unit_banks = stack.enter_context(tc.psum_pool(name="unit_banks", bufs=PER_CHUNK))
+        tile_banks = stack.enter_context(tc.psum_pool(name="tile_banks", bufs=PER_CHUNK))
 
         h_raw = []
         for b in range(B):
@@ -67,10 +71,10 @@ def tile_attentivestatspool_pb_kernel(tc, h, x, mask, w2_words, w2_scales, b2, g
         nc.sync.dma_start(
             out=w_words[:].bitcast(I32), in_=w2_words.rearrange("g p n -> (g p) n").bitcast(I32)
         )
-        for quadrant in range(4):
+        for quadrant in range(P // QUADRANT):
             nc.sync.dma_start(
-                out=w_planes[32 * quadrant : 32 * quadrant + 4, :].bitcast(I32),
-                in_=w2_scales[0, 4 * quadrant : 4 * quadrant + 4, :].bitcast(I32),
+                out=w_planes[QUADRANT * quadrant : QUADRANT * quadrant + PACK, :].bitcast(I32),
+                in_=w2_scales[0, PACK * quadrant : PACK * (quadrant + 1), :].bitcast(I32),
             )
         for b in range(1, B):
             load_h(b)
@@ -80,7 +84,7 @@ def tile_attentivestatspool_pb_kernel(tc, h, x, mask, w2_words, w2_scales, b2, g
         vector_rows = keep.tile([P, P], BF16)
         nc.gpsimd.memset(vector_rows[:], 0.0)
         nc.scalar.dma_start(
-            out=vector_rows[MASK_AT : MASK_AT + B * T_TILES, :],
+            out=vector_rows[MASK_AT : MASK_AT + MASK_COLS, :],
             in_=mask.rearrange("b o (tt p) -> (b o tt) p", p=P),
         )
         nc.scalar.dma_start(out=vector_rows[0:V_COLS, :], in_=g2.rearrange("(j p) -> j p", p=P))
@@ -120,12 +124,12 @@ def tile_attentivestatspool_pb_kernel(tc, h, x, mask, w2_words, w2_scales, b2, g
         nc.scalar.copy(out=vector_rows_f32[:], in_=vector_rows[:])
         vector_bank = unit_banks.tile([P, P], F32, tag="logits")
         nc.tensor.transpose(vector_bank[:], vector_rows_f32[:], identity[:])
-        vectors = keep.tile([P, MASK_AT + B * T_TILES], F32)
-        nc.scalar.copy(out=vectors[:], in_=vector_bank[:, 0 : MASK_AT + B * T_TILES])
+        vectors = keep.tile([P, MASK_AT + MASK_COLS], F32)
+        nc.scalar.copy(out=vectors[:], in_=vector_bank[:, 0 : MASK_AT + MASK_COLS])
         gain = vectors[:, 0:V_COLS]
         bias = vectors[:, V_COLS : 2 * V_COLS]
-        mask_one = vectors[:, MASK_AT : MASK_AT + B * T_TILES]
-        mask_bias = keep.tile([P, B * T_TILES], F32)
+        mask_one = vectors[:, MASK_AT : MASK_AT + MASK_COLS]
+        mask_bias = keep.tile([P, MASK_COLS], F32)
         nc.vector.tensor_scalar(
             out=mask_bias[:], in0=mask_one, scalar1=1.0, scalar2=HUGE, op0=ALU.subtract, op1=ALU.mult
         )
@@ -154,7 +158,7 @@ def tile_attentivestatspool_pb_kernel(tc, h, x, mask, w2_words, w2_scales, b2, g
 
         def unit_logits(u):
             b, rest = divmod(u, C_TILES)
-            cc, tt = divmod(rest, T_TILES)
+            cc, tt = divmod(rest, PER_CHUNK)
             logits = unit_banks.tile([P, C_CHUNK], F32)
             nc.tensor.matmul_mx(
                 out=logits[:],
@@ -168,7 +172,7 @@ def tile_attentivestatspool_pb_kernel(tc, h, x, mask, w2_words, w2_scales, b2, g
             unit_bank[u] = logits
 
         def unit_mask(u):
-            column = T_TILES * (u // C_TILES) + u % T_TILES
+            column = PER_CHUNK * (u // C_TILES) + u % PER_CHUNK
             am_t = units.tile([P, C_CHUNK], F32)
             nc.scalar.activation(
                 out=am_t[:], in_=unit_bank[u][:], func=ACT.Identity,
@@ -177,10 +181,10 @@ def tile_attentivestatspool_pb_kernel(tc, h, x, mask, w2_words, w2_scales, b2, g
             unit_sb[u] = am_t
 
         def tile_transposes(i):
-            first_unit = T_TILES * (i // T_TILES)
-            cl = i % T_TILES
+            first_unit = PER_CHUNK * (i // PER_CHUNK)
+            cl = i % PER_CHUNK
             am = tile_banks.tile([P, T], F32)
-            for tt in range(T_TILES):
+            for tt in range(PER_CHUNK):
                 nc.tensor.transpose(
                     am[:, P * tt : P * (tt + 1)],
                     unit_sb[first_unit + tt][:, P * cl : P * (cl + 1)],
@@ -230,29 +234,29 @@ def tile_attentivestatspool_pb_kernel(tc, h, x, mask, w2_words, w2_scales, b2, g
 
         def members(n):
             if 0 <= n < N_CHUNKS:
-                return list(range(T_TILES * n, T_TILES * (n + 1)))
+                return list(range(PER_CHUNK * n, PER_CHUNK * (n + 1)))
             return []
 
         def gpsimd_share(n):
-            if n + 2 < N_CHUNKS:
-                return members(n)[T_TILES - GPSIMD_TILES :]
+            if n + 1 < N_CHUNKS:
+                return members(n)[PER_CHUNK - GPSIMD_TILES :]
             return []
 
         def vector_share(n):
-            return members(n)[: T_TILES - len(gpsimd_share(n))]
+            return members(n)[: PER_CHUNK - len(gpsimd_share(n))]
 
-        for r in range(-3, N_CHUNKS + 1):
-            for u in members(r + 3):
+        for r in range(-UNITS_AHEAD, N_CHUNKS + 1):
+            for u in members(r + UNITS_AHEAD):
                 unit_logits(u)
-            for i in members(r + 2):
+            for i in members(r + TILES_AHEAD):
                 tile_transposes(i)
-            for i in members(r + 1):
+            for i in members(r):
                 maximum(i)
-            for i in members(r + 1):
+            for i in members(r):
                 weights(i)
             for i in gpsimd_share(r - 1):
                 second_moment_sum(i)
-            for u in members(r + 3):
+            for u in members(r + UNITS_AHEAD):
                 unit_mask(u)
             for i in vector_share(r):
                 first_moment(i)
@@ -264,8 +268,10 @@ def tile_attentivestatspool_pb_kernel(tc, h, x, mask, w2_words, w2_scales, b2, g
 
         by_chunk = "p (n cl) -> p n cl"
         nc.vector.tensor_copy(
-            out=s2[:].rearrange(by_chunk, cl=T_TILES)[:, 0 : N_CHUNKS - 2, T_TILES - GPSIMD_TILES :],
-            in_=s2_scalar[:].rearrange(by_chunk, cl=T_TILES)[:, 0 : N_CHUNKS - 2, T_TILES - GPSIMD_TILES :],
+            out=s2[:].rearrange(by_chunk, cl=PER_CHUNK)[:, 0 : N_CHUNKS - 1, PER_CHUNK - GPSIMD_TILES :],
+            in_=s2_scalar[:].rearrange(by_chunk, cl=PER_CHUNK)[
+                :, 0 : N_CHUNKS - 1, PER_CHUNK - GPSIMD_TILES :
+            ],
         )
         by_b = "p (b c) -> p b c"
         inv_s0 = keep.tile([P, N_TILES], F32)
@@ -334,5 +340,7 @@ def tile_attentivestatspool_pb_kernel(tc, h, x, mask, w2_words, w2_scales, b2, g
         out_rows = keep.tile([P, P], F32)
         nc.vector.tensor_copy(out=out_rows[:], in_=result_bank[:])
         out_view = out.rearrange("b (j p) o -> (b j) (p o)", p=P)
-        nc.sync.dma_start(out=out_view[0:64, :], in_=out_rows[0:64, :])
-        nc.sync.dma_start(out=out_view[64 : B * V_COLS, :], in_=out_rows[64 : B * V_COLS, :])
+        nc.sync.dma_start(out=out_view[0:STORE_SPLIT, :], in_=out_rows[0:STORE_SPLIT, :])
+        nc.sync.dma_start(
+            out=out_view[STORE_SPLIT : B * V_COLS, :], in_=out_rows[STORE_SPLIT : B * V_COLS, :]
+        )

@@ -94,6 +94,8 @@ def tile_attentivestatspool_pb_kernel(tc, h, x, mask, w2_words, w2_scales, b2, g
 
         identity = keep.tile([P, P], F32)
         make_identity(nc, identity[:])
+        identity_bf16 = keep.tile([P, P], BF16)
+        make_identity(nc, identity_bf16[:])
         ones = keep.tile([P, P], F32)
         nc.gpsimd.memset(ones[:], 1.0)
         result = keep.tile([P, P], F32)
@@ -146,6 +148,9 @@ def tile_attentivestatspool_pb_kernel(tc, h, x, mask, w2_words, w2_scales, b2, g
         s1 = keep.tile([P, N_TILES], F32)
         s2 = keep.tile([P, N_TILES], F32)
         s2_scalar = keep.tile([P, N_TILES], F32)
+        nc.gpsimd.memset(s2[:], 0.0)
+        nc.gpsimd.memset(s2_scalar[:], 0.0)
+        x_psum = {}
         unit_bank = {}
         unit_sb = {}
         masked = {}
@@ -205,10 +210,21 @@ def tile_attentivestatspool_pb_kernel(tc, h, x, mask, w2_words, w2_scales, b2, g
             )
             weight[i] = e
 
+        def x_to_psum(early, late):
+            bank = unit_banks.tile([P, 2, T], BF16, tag="logits")
+            for half, i in ((0, late), (1, early)):
+                nc.tensor.matmul(
+                    out=bank[:, half, :], lhsT=identity_bf16[:], rhs=x_tile(i), start=True, stop=True
+                )
+                x_psum[i] = bank[:, half, :]
+
+        def x_for_vector(i):
+            return x_psum.get(i, x_tile(i))
+
         def first_moment(i):
             y = work.tile([P, T], F32)
             nc.vector.scalar_tensor_tensor(
-                out=y[:], in0=weight[i][:], scalar=1.0, in1=x_tile(i), op0=ALU.mult, op1=ALU.mult,
+                out=y[:], in0=weight[i][:], scalar=1.0, in1=x_for_vector(i), op0=ALU.mult, op1=ALU.mult,
                 accum_out=s1[:, i : i + 1],
             )
             weighted[i] = y
@@ -216,7 +232,7 @@ def tile_attentivestatspool_pb_kernel(tc, h, x, mask, w2_words, w2_scales, b2, g
         def second_moment(i):
             unused = scratch.tile([P, T], BF16)
             nc.vector.scalar_tensor_tensor(
-                out=unused[:], in0=weighted[i][:], scalar=1.0, in1=x_tile(i), op0=ALU.mult,
+                out=unused[:], in0=weighted[i][:], scalar=1.0, in1=x_for_vector(i), op0=ALU.mult,
                 op1=ALU.mult, accum_out=s2[:, i : i + 1],
             )
 
@@ -238,41 +254,51 @@ def tile_attentivestatspool_pb_kernel(tc, h, x, mask, w2_words, w2_scales, b2, g
             return []
 
         def gpsimd_share(n):
-            if n + 1 < N_CHUNKS:
-                return members(n)[PER_CHUNK - GPSIMD_TILES :]
-            return []
+            if n == N_CHUNKS - 1:
+                return members(n)[:GPSIMD_TILES]
+            if n == N_CHUNKS - 2:
+                return members(n)
+            return members(n)[PER_CHUNK - GPSIMD_TILES :]
 
         def vector_share(n):
-            return members(n)[: PER_CHUNK - len(gpsimd_share(n))]
+            return [i for i in members(n) if i not in gpsimd_share(n)]
 
         for r in range(-UNITS_AHEAD, N_CHUNKS + 1):
             for u in members(r + UNITS_AHEAD):
                 unit_logits(u)
+            if r == N_CHUNKS - 2:
+                for early, late in zip(members(r), members(r + 1)):
+                    x_to_psum(early, late)
             for i in members(r + TILES_AHEAD):
                 tile_transposes(i)
             for i in members(r):
                 maximum(i)
+            sums_due = gpsimd_share(r - 1)
+            if r == N_CHUNKS - 1:
+                for i in sums_due[:GPSIMD_TILES]:
+                    second_moment_sum(i)
+                sums_due = sums_due[GPSIMD_TILES:]
             for i in members(r):
                 weights(i)
-            for i in gpsimd_share(r - 1):
+            for i in sums_due:
                 second_moment_sum(i)
             for u in members(r + UNITS_AHEAD):
                 unit_mask(u)
+            if r == N_CHUNKS - 1:
+                for i in gpsimd_share(r):
+                    first_moment(i)
+                    second_moment_products(i)
             for i in vector_share(r):
                 first_moment(i)
             for i in vector_share(r):
                 second_moment(i)
-            for i in gpsimd_share(r):
-                first_moment(i)
-                second_moment_products(i)
+            if r < N_CHUNKS - 1:
+                for i in gpsimd_share(r):
+                    first_moment(i)
+                    second_moment_products(i)
 
-        by_chunk = "p (n cl) -> p n cl"
-        nc.vector.tensor_copy(
-            out=s2[:].rearrange(by_chunk, cl=PER_CHUNK)[:, 0 : N_CHUNKS - 1, PER_CHUNK - GPSIMD_TILES :],
-            in_=s2_scalar[:].rearrange(by_chunk, cl=PER_CHUNK)[
-                :, 0 : N_CHUNKS - 1, PER_CHUNK - GPSIMD_TILES :
-            ],
-        )
+        s2_all = keep.tile([P, N_TILES], F32)
+        nc.vector.tensor_tensor(out=s2_all[:], in0=s2[:], in1=s2_scalar[:], op=ALU.add)
         by_b = "p (b c) -> p b c"
         inv_s0 = keep.tile([P, N_TILES], F32)
         nc.vector.reciprocal(out=inv_s0[:], in_=s0[:])
@@ -285,7 +311,7 @@ def tile_attentivestatspool_pb_kernel(tc, h, x, mask, w2_words, w2_scales, b2, g
         nc.vector.tensor_tensor(out=mean_sq[:], in0=mean, in1=mean, op=ALU.mult)
         second = keep.tile([P, B, C_TILES], F32)
         nc.vector.tensor_tensor(
-            out=second[:], in0=s2[:].rearrange(by_b, b=B), in1=inv_s0[:].rearrange(by_b, b=B),
+            out=second[:], in0=s2_all[:].rearrange(by_b, b=B), in1=inv_s0[:].rearrange(by_b, b=B),
             op=ALU.mult,
         )
         var = keep.tile([P, B, C_TILES], F32)

@@ -33,6 +33,7 @@ HUGE = 3.0e38
 GPSIMD_TILES = 2
 UNITS_AHEAD = 2
 TILES_AHEAD = 1
+UNIT_BANKS = 3
 STORE_SPLIT = 64
 
 FLOPS = 2 * B * C * T * H
@@ -46,8 +47,9 @@ def tile_attentivestatspool_pb_kernel(tc, h, x, mask, w2_words, w2_scales, b2, g
         units = stack.enter_context(tc.tile_pool(name="units", bufs=2 * PER_CHUNK))
         work = stack.enter_context(tc.tile_pool(name="work", bufs=2 * PER_CHUNK))
         scratch = stack.enter_context(tc.tile_pool(name="scratch", bufs=2 * GPSIMD_TILES))
-        unit_banks = stack.enter_context(tc.psum_pool(name="unit_banks", bufs=PER_CHUNK))
+        unit_banks = stack.enter_context(tc.psum_pool(name="unit_banks", bufs=UNIT_BANKS))
         tile_banks = stack.enter_context(tc.psum_pool(name="tile_banks", bufs=PER_CHUNK))
+        x_banks = stack.enter_context(tc.psum_pool(name="x_banks", bufs=1))
 
         h_raw = []
         for b in range(B):
@@ -210,9 +212,9 @@ def tile_attentivestatspool_pb_kernel(tc, h, x, mask, w2_words, w2_scales, b2, g
             )
             weight[i] = e
 
-        def x_to_psum(early, late):
-            bank = unit_banks.tile([P, 2, T], BF16, tag="logits")
-            for half, i in ((0, late), (1, early)):
+        def x_to_psum(pool, tiles):
+            bank = pool.tile([P, 2, T], BF16, tag="logits")
+            for half, i in enumerate(tiles):
                 nc.tensor.matmul(
                     out=bank[:, half, :], lhsT=identity_bf16[:], rhs=x_tile(i), start=True, stop=True
                 )
@@ -264,13 +266,19 @@ def tile_attentivestatspool_pb_kernel(tc, h, x, mask, w2_words, w2_scales, b2, g
             return [i for i in members(n) if i not in gpsimd_share(n)]
 
         for r in range(-UNITS_AHEAD, N_CHUNKS + 1):
-            for u in members(r + UNITS_AHEAD):
+            for u in members(r + UNITS_AHEAD)[:UNIT_BANKS]:
                 unit_logits(u)
             if r == N_CHUNKS - 2:
-                for early, late in zip(members(r), members(r + 1)):
-                    x_to_psum(early, late)
+                for early, late in list(zip(members(r), members(r + 1)))[1:]:
+                    x_to_psum(unit_banks, [late, early])
             for i in members(r + TILES_AHEAD):
                 tile_transposes(i)
+            if 1 <= r + 1 < N_CHUNKS - 2:
+                x_to_psum(x_banks, members(r + 1)[:1])
+            if r + 1 == N_CHUNKS - 2:
+                x_to_psum(x_banks, [members(r + 2)[0], members(r + 1)[0]])
+            for u in members(r + UNITS_AHEAD)[UNIT_BANKS:]:
+                unit_logits(u)
             for i in members(r):
                 maximum(i)
             sums_due = gpsimd_share(r - 1)

@@ -149,9 +149,14 @@ def tile_attentivestatspool_pb_kernel(tc, h, x, mask, w2_words, w2_scales, b2, g
         s0 = keep.tile([P, N_TILES], F32)
         s1 = keep.tile([P, N_TILES], F32)
         s2 = keep.tile([P, N_TILES], F32)
-        s2_scalar = keep.tile([P, N_TILES], F32)
-        nc.gpsimd.memset(s2[:], 0.0)
-        nc.gpsimd.memset(s2_scalar[:], 0.0)
+        by_b = "p (b c) -> p b c"
+        inv_s0 = keep.tile([P, N_TILES], F32)
+        pooled = keep.tile([P, B, 2, C_TILES], F32)
+        mean = pooled[:, :, 0, :]
+        mean_sq = keep.tile([P, B, C_TILES], F32)
+        sums_vector = keep.tile([P, 2 * B], F32)
+        sums_scalar = keep.tile([P, 2 * B], F32)
+        nc.gpsimd.memset(sums_scalar[:], 0.0)
         x_psum = {}
         unit_bank = {}
         unit_sb = {}
@@ -247,7 +252,15 @@ def tile_attentivestatspool_pb_kernel(tc, h, x, mask, w2_words, w2_scales, b2, g
             unused_sum = scratch.tile([P, T], BF16)
             nc.scalar.activation(
                 out=unused_sum[:], in_=weighted_sq[i][:], func=ACT.Copy,
-                accum_out=s2_scalar[:, i : i + 1],
+                accum_out=s2[:, i : i + 1],
+            )
+
+        def invert_s0():
+            nc.vector.reciprocal(out=inv_s0[:], in_=s0[:])
+
+        def means():
+            nc.vector.tensor_tensor(
+                out=mean, in0=s1[:].rearrange(by_b, b=B), in1=inv_s0[:].rearrange(by_b, b=B), op=ALU.mult
             )
 
         def members(n):
@@ -298,54 +311,51 @@ def tile_attentivestatspool_pb_kernel(tc, h, x, mask, w2_words, w2_scales, b2, g
                     second_moment_products(i)
             for i in vector_share(r):
                 first_moment(i)
-            for i in vector_share(r):
+            between = [invert_s0, means] if r == N_CHUNKS - 1 else []
+            for n, i in enumerate(vector_share(r)):
+                for step in between[n : n + 1]:
+                    step()
                 second_moment(i)
             if r < N_CHUNKS - 1:
                 for i in gpsimd_share(r):
                     first_moment(i)
                     second_moment_products(i)
 
-        s2_all = keep.tile([P, N_TILES], F32)
-        nc.vector.tensor_tensor(out=s2_all[:], in0=s2[:], in1=s2_scalar[:], op=ALU.add)
-        by_b = "p (b c) -> p b c"
-        inv_s0 = keep.tile([P, N_TILES], F32)
-        nc.vector.reciprocal(out=inv_s0[:], in_=s0[:])
-        pooled = keep.tile([P, B, 2, C_TILES], F32)
-        mean = pooled[:, :, 0, :]
-        nc.vector.tensor_tensor(
-            out=mean, in0=s1[:].rearrange(by_b, b=B), in1=inv_s0[:].rearrange(by_b, b=B), op=ALU.mult
-        )
-        mean_sq = keep.tile([P, B, C_TILES], F32)
         nc.vector.tensor_tensor(out=mean_sq[:], in0=mean, in1=mean, op=ALU.mult)
         second = keep.tile([P, B, C_TILES], F32)
         nc.vector.tensor_tensor(
-            out=second[:], in0=s2_all[:].rearrange(by_b, b=B), in1=inv_s0[:].rearrange(by_b, b=B),
-            op=ALU.mult,
+            out=second[:], in0=s2[:].rearrange(by_b, b=B), in1=inv_s0[:].rearrange(by_b, b=B), op=ALU.mult
         )
+        mean_sq_floor = keep.tile([P, B, C_TILES], F32)
+        nc.vector.tensor_scalar_add(out=mean_sq_floor[:], in0=mean_sq[:], scalar1=EPS_STD)
         var = keep.tile([P, B, C_TILES], F32)
         nc.vector.tensor_tensor(out=var[:], in0=second[:], in1=mean_sq[:], op=ALU.subtract)
+        squares = keep.tile([P, B, C_TILES], F32)
+        nc.vector.tensor_tensor(out=squares[:], in0=second[:], in1=mean_sq_floor[:], op=ALU.max)
         var_floor = keep.tile([P, B, C_TILES], F32)
         nc.vector.tensor_scalar_max(out=var_floor[:], in0=var[:], scalar1=EPS_STD)
-        nc.scalar.activation(out=pooled[:, :, 1, :], in_=var_floor[:], func=ACT.Sqrt)
+        for b in range(B):
+            nc.scalar.activation(
+                out=pooled[:, b, 1, :], in_=var_floor[:, b, :], func=ACT.Sqrt,
+                accum_out=sums_scalar[:, b : b + 1],
+            )
 
-        sums = keep.tile([P, 2 * B], F32)
-        squares = keep.tile([P, B, C_TILES], F32)
-        nc.vector.tensor_tensor(out=squares[:], in0=mean_sq[:], in1=var_floor[:], op=ALU.add)
-        nc.vector.tensor_reduce(out=sums[:, B : 2 * B], in_=squares[:], axis=AX.X, op=ALU.add)
-        pooled_rows = pooled[:].rearrange("p b s c -> p b (s c)")
-        nc.vector.tensor_reduce(out=sums[:, 0:B], in_=pooled_rows, axis=AX.X, op=ALU.add)
+        nc.vector.tensor_reduce(out=sums_vector[:, B : 2 * B], in_=squares[:], axis=AX.X, op=ALU.add)
+        nc.vector.tensor_reduce(out=sums_vector[:, 0:B], in_=mean, axis=AX.X, op=ALU.add)
         totals = unit_banks.tile([P, 2 * B], F32, tag="logits")
-        nc.tensor.matmul(out=totals[:], lhsT=ones[:], rhs=sums[:], start=True, stop=True)
+        nc.tensor.matmul(out=totals[:], lhsT=ones[:], rhs=sums_vector[:], start=True, stop=False)
+        nc.tensor.matmul(out=totals[:], lhsT=ones[:], rhs=sums_scalar[:], start=False, stop=True)
         moments = keep.tile([P, 2 * B], F32)
         nc.vector.tensor_scalar_mul(out=moments[:], in0=totals[:], scalar1=1.0 / (2 * C))
         mu = moments[:, 0:B]
         wide = [P, B, V_COLS]
+        mu_sq = keep.tile([P, B], F32)
+        nc.vector.tensor_tensor(out=mu_sq[:], in0=mu, in1=mu, op=ALU.mult)
+        pooled_rows = pooled[:].rearrange("p b s c -> p b (s c)")
         centred = keep.tile(wide, F32)
         nc.vector.tensor_tensor(
             out=centred[:], in0=pooled_rows, in1=mu.unsqueeze(2).to_broadcast(wide), op=ALU.subtract
         )
-        mu_sq = keep.tile([P, B], F32)
-        nc.vector.tensor_tensor(out=mu_sq[:], in0=mu, in1=mu, op=ALU.mult)
         ln_var = keep.tile([P, B], F32)
         nc.vector.scalar_tensor_tensor(
             out=ln_var[:], in0=moments[:, B : 2 * B], scalar=EPS_LN, in1=mu_sq[:],
@@ -360,14 +370,11 @@ def tile_attentivestatspool_pb_kernel(tc, h, x, mask, w2_words, w2_scales, b2, g
         )
         inv_std = keep.tile([P, B], F32)
         nc.vector.reciprocal(out=inv_std[:], in_=ln_std[:])
-        scaled = keep.tile(wide, F32)
-        nc.vector.tensor_tensor(
-            out=scaled[:], in0=gained[:], in1=inv_std[:].unsqueeze(2).to_broadcast(wide), op=ALU.mult
-        )
-        nc.vector.tensor_tensor(
-            out=result[:, 0 : B * V_COLS].rearrange("p (b j) -> p b j", b=B), in0=scaled[:],
-            in1=bias.unsqueeze(1).to_broadcast(wide), op=ALU.add,
-        )
+        for b in range(B):
+            nc.vector.scalar_tensor_tensor(
+                out=result[:, V_COLS * b : V_COLS * (b + 1)], in0=gained[:, b, :],
+                scalar=inv_std[:, b : b + 1], in1=bias, op0=ALU.mult, op1=ALU.add,
+            )
 
         result_bank = unit_banks.tile([P, P], F32, tag="logits")
         nc.tensor.transpose(result_bank[:], result[:], identity[:])
@@ -375,6 +382,6 @@ def tile_attentivestatspool_pb_kernel(tc, h, x, mask, w2_words, w2_scales, b2, g
         nc.vector.tensor_copy(out=out_rows[:], in_=result_bank[:])
         out_view = out.rearrange("b (j p) o -> (b j) (p o)", p=P)
         nc.sync.dma_start(out=out_view[0:STORE_SPLIT, :], in_=out_rows[0:STORE_SPLIT, :])
-        nc.sync.dma_start(
+        nc.scalar.dma_start(
             out=out_view[STORE_SPLIT : B * V_COLS, :], in_=out_rows[STORE_SPLIT : B * V_COLS, :]
         )

@@ -47,6 +47,7 @@ def tile_attentivestatspool_pb_kernel(tc, h, x, mask, w2_words, w2_scales, b2, g
         units = stack.enter_context(tc.tile_pool(name="units", bufs=2 * PER_CHUNK))
         work = stack.enter_context(tc.tile_pool(name="work", bufs=2 * PER_CHUNK))
         scratch = stack.enter_context(tc.tile_pool(name="scratch", bufs=2 * GPSIMD_TILES))
+        grouped = stack.enter_context(tc.tile_pool(name="grouped", bufs=1))
         unit_banks = stack.enter_context(tc.psum_pool(name="unit_banks", bufs=UNIT_BANKS))
         tile_banks = stack.enter_context(tc.psum_pool(name="tile_banks", bufs=PER_CHUNK))
         x_banks = stack.enter_context(tc.psum_pool(name="x_banks", bufs=1))
@@ -61,8 +62,15 @@ def tile_attentivestatspool_pb_kernel(tc, h, x, mask, w2_words, w2_scales, b2, g
         w_planes = keep.tile([P, C], U8, align_bytes=64)
         nc.vector.memset(w_planes[:].bitcast(I32), 0)
 
-        def load_h(b):
-            nc.sync.dma_start(out=h_raw[b][:], in_=h[b].rearrange("(p j) t -> p j t", j=PACK))
+        def load_h(b, first=0, last=T):
+            rows = h[b].rearrange("(p j) t -> p j t", j=PACK)
+            nc.sync.dma_start(out=h_raw[b][:, :, first:last], in_=rows[:, :, first:last])
+
+        def load_words(first, last):
+            nc.sync.dma_start(
+                out=w_words[:, first:last].bitcast(I32),
+                in_=w2_words.rearrange("g p n -> (g p) n")[:, first:last].bitcast(I32),
+            )
 
         def load_x(i):
             b, first = divmod(i * X_GROUP, C_TILES)
@@ -70,21 +78,21 @@ def tile_attentivestatspool_pb_kernel(tc, h, x, mask, w2_words, w2_scales, b2, g
             nc.sync.dma_start(out=x_sb[i][:], in_=rows[:, first : first + X_GROUP, :])
 
         load_h(0)
-        nc.sync.dma_start(
-            out=w_words[:].bitcast(I32), in_=w2_words.rearrange("g p n -> (g p) n").bitcast(I32)
-        )
+        load_words(0, 2 * C)
         for quadrant in range(P // QUADRANT):
             nc.sync.dma_start(
                 out=w_planes[QUADRANT * quadrant : QUADRANT * quadrant + PACK, :].bitcast(I32),
                 in_=w2_scales[0, PACK * quadrant : PACK * (quadrant + 1), :].bitcast(I32),
             )
-        for b in range(1, B):
-            load_h(b)
-        for i in range(N_TILES // X_GROUP):
+        load_h(1)
+        load_h(2)
+        load_x(0)
+        load_h(3)
+        for i in range(1, N_TILES // X_GROUP):
             load_x(i)
 
         vector_rows = keep.tile([P, P], BF16)
-        nc.gpsimd.memset(vector_rows[:], 0.0)
+        nc.gpsimd.memset(vector_rows[MASK_AT + MASK_COLS : P, :], 0.0)
         nc.scalar.dma_start(
             out=vector_rows[MASK_AT : MASK_AT + MASK_COLS, :],
             in_=mask.rearrange("b o (tt p) -> (b o tt) p", p=P),
@@ -94,10 +102,10 @@ def tile_attentivestatspool_pb_kernel(tc, h, x, mask, w2_words, w2_scales, b2, g
             out=vector_rows[V_COLS : 2 * V_COLS, :], in_=be2.rearrange("(j p) -> j p", p=P)
         )
 
-        identity = keep.tile([P, P], F32)
-        make_identity(nc, identity[:])
         identity_bf16 = keep.tile([P, P], BF16)
         make_identity(nc, identity_bf16[:])
+        identity = keep.tile([P, P], F32)
+        make_identity(nc, identity[:])
         ones = keep.tile([P, P], F32)
         nc.gpsimd.memset(ones[:], 1.0)
         result = keep.tile([P, P], F32)
@@ -105,45 +113,57 @@ def tile_attentivestatspool_pb_kernel(tc, h, x, mask, w2_words, w2_scales, b2, g
 
         h_codes = keep.tile([P, B, T], U32, align_bytes=64)
         h_planes = keep.tile([P, B, T], U8, align_bytes=64)
-        h_grouped = []
-        for b in range(B):
-            h_grouped.append(keep.tile([P, T, PACK], BF16, name="h_grouped_%d" % b, align_bytes=64))
+        first_grouped = keep.tile([P, T, PACK], BF16, align_bytes=64)
+        h_grouped = {0: first_grouped}
 
-        def regroup_h(b):
+        def next_grouped(b):
+            later_grouped = grouped.tile([P, T, PACK], BF16, align_bytes=64)
+            h_grouped[b] = later_grouped
+
+        def regroup_h_gpsimd(b):
+            nc.gpsimd.tensor_scalar(
+                out=h_grouped[b][:], in0=h_raw[b][:].rearrange("p j t -> p t j"), scalar1=1.0,
+                scalar2=0.0, op0=ALU.mult, op1=ALU.add,
+            )
+
+        def regroup_h(b, first=0, last=T):
             nc.vector.tensor_copy(
-                out=h_grouped[b][:].rearrange("p (c i) j -> p c j i", i=4),
-                in_=h_raw[b][:].rearrange("p j (c i) -> p c j i", i=4),
+                out=h_grouped[b][:, first:last, :].rearrange("p (c i) j -> p c j i", i=4),
+                in_=h_raw[b][:, :, first:last].rearrange("p j (c i) -> p c j i", i=4),
             )
 
-        def quantise_h(b):
+        def quantise_h(b, first=0, last=T):
             nc.vector.quantize_mx(
-                out=h_codes[:, b, :].bitcast(FP8X4),
-                scales=h_planes[:, b, :],
-                in_=h_grouped[b][:].rearrange("p t j -> p (t j)"),
+                out=h_codes[:, b, first:last].bitcast(FP8X4),
+                scales=h_planes[:, b, first:last],
+                in_=h_grouped[b][:, first:last, :].rearrange("p t j -> p (t j)"),
             )
 
-        regroup_h(0)
-
-        vector_rows_f32 = keep.tile([P, P], F32)
-        nc.scalar.copy(out=vector_rows_f32[:], in_=vector_rows[:])
-        vector_bank = unit_banks.tile([P, P], F32, tag="logits")
-        nc.tensor.transpose(vector_bank[:], vector_rows_f32[:], identity[:])
-        vectors = keep.tile([P, MASK_AT + MASK_COLS], F32)
-        nc.scalar.copy(out=vectors[:], in_=vector_bank[:, 0 : MASK_AT + MASK_COLS])
+        vector_bank = unit_banks.tile([P, P], BF16, tag="logits")
+        nc.tensor.transpose(vector_bank[:], vector_rows[:], identity_bf16[:])
+        vectors = keep.tile([P, MASK_AT], F32)
+        nc.scalar.copy(out=vectors[:], in_=vector_bank[:, 0:MASK_AT])
         gain = vectors[:, 0:V_COLS]
         bias = vectors[:, V_COLS : 2 * V_COLS]
-        mask_one = vectors[:, MASK_AT : MASK_AT + MASK_COLS]
         mask_bias = keep.tile([P, MASK_COLS], F32)
-        nc.vector.tensor_scalar(
-            out=mask_bias[:], in0=mask_one, scalar1=1.0, scalar2=HUGE, op0=ALU.subtract, op1=ALU.mult
-        )
 
-        quantise_h(0)
+        regroup_h(0, 0, P)
+        regroup_h(0, P, 2 * P)
+        quantise_h(0, 0, P)
+        nc.vector.tensor_scalar(
+            out=mask_bias[:], in0=vector_bank[:, MASK_AT : MASK_AT + MASK_COLS], scalar1=1.0,
+            scalar2=HUGE, op0=ALU.subtract, op1=ALU.mult,
+        )
+        for tt in range(2, PER_CHUNK):
+            regroup_h(0, P * tt, P * (tt + 1))
+            quantise_h(0, P * (tt - 1), P * tt)
+        next_grouped(1)
         regroup_h(1)
-        for b in range(2, B):
-            regroup_h(b)
-            quantise_h(b - 1)
-        quantise_h(B - 1)
+        quantise_h(0, P * (PER_CHUNK - 1), T)
+        quantise_h(1)
+        next_grouped(2)
+        regroup_h_gpsimd(2)
+        late_h = {2: (quantise_h, 2), 3: (regroup_h, 3), 4: (quantise_h, 3)}
 
         neg_max = keep.tile([P, N_TILES], F32)
         s0 = keep.tile([P, N_TILES], F32)
@@ -188,7 +208,7 @@ def tile_attentivestatspool_pb_kernel(tc, h, x, mask, w2_words, w2_scales, b2, g
             am_t = units.tile([P, C_CHUNK], F32)
             nc.scalar.activation(
                 out=am_t[:], in_=unit_bank[u][:], func=ACT.Identity,
-                bias=mask_bias[:, column : column + 1], scale=mask_one[:, column : column + 1],
+                bias=mask_bias[:, column : column + 1], scale=1.0,
             )
             unit_sb[u] = am_t
 
@@ -292,6 +312,8 @@ def tile_attentivestatspool_pb_kernel(tc, h, x, mask, w2_words, w2_scales, b2, g
                 x_to_psum(x_banks, [members(r + 2)[0], members(r + 1)[0]])
             for u in members(r + UNITS_AHEAD)[UNIT_BANKS:]:
                 unit_logits(u)
+            if r + 1 == 0:
+                x_to_psum(x_banks, members(r + 1)[:1])
             for i in members(r):
                 maximum(i)
             sums_due = gpsimd_share(r - 1)
@@ -316,6 +338,11 @@ def tile_attentivestatspool_pb_kernel(tc, h, x, mask, w2_words, w2_scales, b2, g
                 for step in between[n : n + 1]:
                     step()
                 second_moment(i)
+                if n == 0 and r in late_h:
+                    step, b = late_h[r]
+                    if step == regroup_h:
+                        next_grouped(b)
+                    step(b)
             if r < N_CHUNKS - 1:
                 for i in gpsimd_share(r):
                     first_moment(i)

@@ -126,6 +126,11 @@ def tile_attentivestatspool_pb_kernel(tc, h, x, mask, w2_words, w2_scales, b2, g
                 scalar2=0.0, op0=ALU.mult, op1=ALU.add,
             )
 
+        def regroup_h_scalar(b, first, last):
+            nc.scalar.copy(
+                out=h_grouped[b][:, first:last, :], in_=h_raw[b][:, :, first:last].rearrange("p j t -> p t j")
+            )
+
         def regroup_h(b, first=0, last=T):
             nc.vector.tensor_copy(
                 out=h_grouped[b][:, first:last, :].rearrange("p (c i) j -> p c j i", i=4),
@@ -142,7 +147,6 @@ def tile_attentivestatspool_pb_kernel(tc, h, x, mask, w2_words, w2_scales, b2, g
         vector_bank = unit_banks.tile([P, P], BF16, tag="logits")
         nc.tensor.transpose(vector_bank[:], vector_rows[:], identity_bf16[:])
         vectors = keep.tile([P, MASK_AT], F32)
-        nc.scalar.copy(out=vectors[:], in_=vector_bank[:, 0:MASK_AT])
         gain = vectors[:, 0:V_COLS]
         bias = vectors[:, V_COLS : 2 * V_COLS]
         mask_bias = keep.tile([P, MASK_COLS], F32)
@@ -155,15 +159,16 @@ def tile_attentivestatspool_pb_kernel(tc, h, x, mask, w2_words, w2_scales, b2, g
             scalar2=HUGE, op0=ALU.subtract, op1=ALU.mult,
         )
         for tt in range(2, PER_CHUNK):
-            regroup_h(0, P * tt, P * (tt + 1))
-            quantise_h(0, P * (tt - 1), P * tt)
+            regroup_h_scalar(0, P * tt, P * (tt + 1))
+        nc.scalar.copy(out=vectors[:], in_=vector_bank[:, 0:MASK_AT])
+        for tt in range(1, PER_CHUNK):
+            quantise_h(0, P * tt, P * (tt + 1))
         next_grouped(1)
         regroup_h(1)
-        quantise_h(0, P * (PER_CHUNK - 1), T)
         quantise_h(1)
         next_grouped(2)
         regroup_h_gpsimd(2)
-        late_h = {2: (quantise_h, 2), 3: (regroup_h, 3), 4: (quantise_h, 3)}
+        late_h = {1: (quantise_h, 2), 6: (quantise_h, 3)}
 
         neg_max = keep.tile([P, N_TILES], F32)
         s0 = keep.tile([P, N_TILES], F32)
@@ -327,6 +332,10 @@ def tile_attentivestatspool_pb_kernel(tc, h, x, mask, w2_words, w2_scales, b2, g
                 second_moment_sum(i)
             for u in members(r + UNITS_AHEAD):
                 unit_mask(u)
+            if 2 <= r < 2 + PER_CHUNK:
+                if r == 2:
+                    next_grouped(3)
+                regroup_h_scalar(3, P * (r - 2), P * (r - 1))
             if r == N_CHUNKS - 1:
                 for i in gpsimd_share(r):
                     first_moment(i)
@@ -340,8 +349,6 @@ def tile_attentivestatspool_pb_kernel(tc, h, x, mask, w2_words, w2_scales, b2, g
                 second_moment(i)
                 if n == 0 and r in late_h:
                     step, b = late_h[r]
-                    if step == regroup_h:
-                        next_grouped(b)
                     step(b)
             if r < N_CHUNKS - 1:
                 for i in gpsimd_share(r):

@@ -34,6 +34,8 @@ GPSIMD_TILES = 2
 UNITS_AHEAD = 2
 TILES_AHEAD = 1
 UNIT_BANKS = 3
+SPLIT_FROM = 4
+HALF = T // 2
 STORE_SPLIT = 64
 
 FLOPS = 2 * B * C * T * H
@@ -46,7 +48,7 @@ def tile_attentivestatspool_pb_kernel(tc, h, x, mask, w2_words, w2_scales, b2, g
         keep = stack.enter_context(tc.tile_pool(name="keep", bufs=1))
         units = stack.enter_context(tc.tile_pool(name="units", bufs=2 * PER_CHUNK))
         work = stack.enter_context(tc.tile_pool(name="work", bufs=2 * PER_CHUNK))
-        scratch = stack.enter_context(tc.tile_pool(name="scratch", bufs=2 * GPSIMD_TILES))
+        scratch = stack.enter_context(tc.tile_pool(name="scratch", bufs=3 * GPSIMD_TILES))
         grouped = stack.enter_context(tc.tile_pool(name="grouped", bufs=1))
         unit_banks = stack.enter_context(tc.psum_pool(name="unit_banks", bufs=UNIT_BANKS))
         tile_banks = stack.enter_context(tc.psum_pool(name="tile_banks", bufs=PER_CHUNK))
@@ -120,9 +122,10 @@ def tile_attentivestatspool_pb_kernel(tc, h, x, mask, w2_words, w2_scales, b2, g
             later_grouped = grouped.tile([P, T, PACK], BF16, align_bytes=64)
             h_grouped[b] = later_grouped
 
-        def regroup_h_gpsimd(b):
+        def regroup_h_gpsimd(b, first=0, last=T):
             nc.gpsimd.tensor_scalar(
-                out=h_grouped[b][:], in0=h_raw[b][:].rearrange("p j t -> p t j"), scalar1=1.0,
+                out=h_grouped[b][:, first:last, :],
+                in0=h_raw[b][:, :, first:last].rearrange("p j t -> p t j"), scalar1=1.0,
                 scalar2=0.0, op0=ALU.mult, op1=ALU.add,
             )
 
@@ -168,7 +171,9 @@ def tile_attentivestatspool_pb_kernel(tc, h, x, mask, w2_words, w2_scales, b2, g
         quantise_h(1)
         next_grouped(2)
         regroup_h_gpsimd(2)
-        late_h = {1: (quantise_h, 2), 6: (quantise_h, 3)}
+        last_grouped = keep.tile([P, T, PACK], BF16, align_bytes=64)
+        h_grouped[3] = last_grouped
+        late_h = {1: (quantise_h, 2), SPLIT_FROM + 1: (quantise_h, 3)}
 
         neg_max = keep.tile([P, N_TILES], F32)
         s0 = keep.tile([P, N_TILES], F32)
@@ -182,6 +187,8 @@ def tile_attentivestatspool_pb_kernel(tc, h, x, mask, w2_words, w2_scales, b2, g
         sums_vector = keep.tile([P, 2 * B], F32)
         sums_scalar = keep.tile([P, 2 * B], F32)
         nc.gpsimd.memset(sums_scalar[:], 0.0)
+        s2_part = keep.tile([P, N_TILES], F32)
+        nc.gpsimd.memset(s2_part[:], 0.0)
         x_psum = {}
         unit_bank = {}
         unit_sb = {}
@@ -261,23 +268,27 @@ def tile_attentivestatspool_pb_kernel(tc, h, x, mask, w2_words, w2_scales, b2, g
             )
             weighted[i] = y
 
-        def second_moment(i):
+        def second_moment(i, first=0):
             unused = scratch.tile([P, T], BF16)
             nc.vector.scalar_tensor_tensor(
-                out=unused[:], in0=weighted[i][:], scalar=1.0, in1=x_for_vector(i), op0=ALU.mult,
-                op1=ALU.mult, accum_out=s2[:, i : i + 1],
+                out=unused[:, first:T], in0=weighted[i][:, first:T], scalar=1.0,
+                in1=x_for_vector(i)[:, first:T], op0=ALU.mult, op1=ALU.mult, accum_out=s2[:, i : i + 1],
             )
 
-        def second_moment_products(i):
+        def second_moment_products(i, last=T):
             y2 = scratch.tile([P, T], F32)
-            nc.gpsimd.tensor_tensor(out=y2[:], in0=weighted[i][:], in1=x_tile(i), op=ALU.mult)
-            weighted_sq[i] = y2
+            nc.gpsimd.tensor_tensor(
+                out=y2[:, 0:last], in0=weighted[i][:, 0:last], in1=x_tile(i)[:, 0:last], op=ALU.mult
+            )
+            weighted_sq[i] = y2[:, 0:last]
 
         def second_moment_sum(i):
             unused_sum = scratch.tile([P, T], BF16)
+            width = weighted_sq[i].shape[1]
+            into = s2 if width == T else s2_part
             nc.scalar.activation(
-                out=unused_sum[:], in_=weighted_sq[i][:], func=ACT.Copy,
-                accum_out=s2[:, i : i + 1],
+                out=unused_sum[:, 0:width], in_=weighted_sq[i], func=ACT.Copy,
+                accum_out=into[:, i : i + 1],
             )
 
         def invert_s0():
@@ -293,15 +304,17 @@ def tile_attentivestatspool_pb_kernel(tc, h, x, mask, w2_words, w2_scales, b2, g
                 return list(range(PER_CHUNK * n, PER_CHUNK * (n + 1)))
             return []
 
-        def gpsimd_share(n):
+        def gpsimd_jobs(n):
+            tiles = members(n)
+            if not tiles:
+                return []
             if n == N_CHUNKS - 1:
-                return members(n)[:GPSIMD_TILES]
+                return tiles[:2]
             if n == N_CHUNKS - 2:
-                return members(n)
-            return members(n)[PER_CHUNK - GPSIMD_TILES :]
-
-        def vector_share(n):
-            return [i for i in members(n) if i not in gpsimd_share(n)]
+                return tiles
+            if n >= SPLIT_FROM:
+                return [tiles[3], tiles[2], tiles[1]]
+            return tiles[:1:-1]
 
         for r in range(-UNITS_AHEAD, N_CHUNKS + 1):
             for u in members(r + UNITS_AHEAD)[:UNIT_BANKS]:
@@ -319,42 +332,64 @@ def tile_attentivestatspool_pb_kernel(tc, h, x, mask, w2_words, w2_scales, b2, g
                 unit_logits(u)
             if r + 1 == 0:
                 x_to_psum(x_banks, members(r + 1)[:1])
-            for i in members(r):
-                maximum(i)
-            sums_due = gpsimd_share(r - 1)
-            if r == N_CHUNKS - 1:
-                for i in sums_due[:GPSIMD_TILES]:
+
+            tiles = members(r)
+            sums_due = gpsimd_jobs(r - 1)
+            if 0 <= r < N_CHUNKS - 2:
+                for i in tiles[:3]:
+                    maximum(i)
+                for i in tiles[:3]:
+                    weights(i)
+                for i in sums_due[:1]:
                     second_moment_sum(i)
-                sums_due = sums_due[GPSIMD_TILES:]
-            for i in members(r):
-                weights(i)
-            for i in sums_due:
-                second_moment_sum(i)
-            for u in members(r + UNITS_AHEAD):
-                unit_mask(u)
-            if 2 <= r < 2 + PER_CHUNK:
-                if r == 2:
-                    next_grouped(3)
-                regroup_h_scalar(3, P * (r - 2), P * (r - 1))
-            if r == N_CHUNKS - 1:
-                for i in gpsimd_share(r):
-                    first_moment(i)
-                    second_moment_products(i)
-            for i in vector_share(r):
-                first_moment(i)
-            between = [invert_s0, means] if r == N_CHUNKS - 1 else []
-            for n, i in enumerate(vector_share(r)):
-                for step in between[n : n + 1]:
-                    step()
-                second_moment(i)
-                if n == 0 and r in late_h:
+                first_moment(tiles[0])
+                maximum(tiles[3])
+                weights(tiles[3])
+                for i in sums_due[1:]:
+                    second_moment_sum(i)
+                for u in members(r + UNITS_AHEAD):
+                    unit_mask(u)
+                second_moment(tiles[0])
+                if r in late_h:
                     step, b = late_h[r]
                     step(b)
-            if r < N_CHUNKS - 1:
-                for i in gpsimd_share(r):
+                first_moment(tiles[1])
+                first_moment(tiles[2])
+                second_moment(tiles[1], HALF if r >= SPLIT_FROM else 0)
+                first_moment(tiles[3])
+                second_moment_products(tiles[3])
+                second_moment_products(tiles[2])
+                if r < SPLIT_FROM:
+                    regroup_h_gpsimd(3, P * r, P * (r + 1))
+                else:
+                    second_moment_products(tiles[1], HALF)
+            else:
+                for u in members(r + UNITS_AHEAD):
+                    unit_mask(u)
+                for i in tiles:
+                    maximum(i)
+                if r == N_CHUNKS - 1:
+                    for i in sums_due[:2]:
+                        second_moment_sum(i)
+                    sums_due = sums_due[2:]
+                for i in tiles:
+                    weights(i)
+                for i in sums_due:
+                    second_moment_sum(i)
+                for i in gpsimd_jobs(r):
                     first_moment(i)
                     second_moment_products(i)
+                own = [i for i in tiles if i not in gpsimd_jobs(r)]
+                for i in own:
+                    first_moment(i)
+                for step, i in zip([invert_s0, means], own):
+                    step()
+                    second_moment(i)
 
+        split_columns = slice(PER_CHUNK * SPLIT_FROM, PER_CHUNK * (N_CHUNKS - 2))
+        nc.vector.tensor_tensor(
+            out=s2[:, split_columns], in0=s2[:, split_columns], in1=s2_part[:, split_columns], op=ALU.add
+        )
         nc.vector.tensor_tensor(out=mean_sq[:], in0=mean, in1=mean, op=ALU.mult)
         second = keep.tile([P, B, C_TILES], F32)
         nc.vector.tensor_tensor(

@@ -35,6 +35,7 @@ UNITS_AHEAD = 2
 TILES_AHEAD = 1
 UNIT_BANKS = 3
 SPLIT_FROM = 4
+SPLIT_CHUNKS = (5, 7, 9)
 HALF = T // 2
 STORE_SPLIT = 64
 
@@ -312,7 +313,7 @@ def tile_attentivestatspool_pb_kernel(tc, h, x, mask, w2_words, w2_scales, b2, g
                 return tiles[:2]
             if n == N_CHUNKS - 2:
                 return tiles
-            if n >= SPLIT_FROM:
+            if n in SPLIT_CHUNKS:
                 return [tiles[3], tiles[2], tiles[1]]
             return tiles[:1:-1]
 
@@ -355,13 +356,13 @@ def tile_attentivestatspool_pb_kernel(tc, h, x, mask, w2_words, w2_scales, b2, g
                     step(b)
                 first_moment(tiles[1])
                 first_moment(tiles[2])
-                second_moment(tiles[1], HALF if r >= SPLIT_FROM else 0)
+                second_moment(tiles[1], HALF if r in SPLIT_CHUNKS else 0)
                 first_moment(tiles[3])
                 second_moment_products(tiles[3])
                 second_moment_products(tiles[2])
                 if r < SPLIT_FROM:
                     regroup_h_gpsimd(3, P * r, P * (r + 1))
-                else:
+                if r in SPLIT_CHUNKS:
                     second_moment_products(tiles[1], HALF)
             else:
                 for u in members(r + UNITS_AHEAD):

@@ -35,7 +35,7 @@ UNITS_AHEAD = 2
 TILES_AHEAD = 1
 UNIT_BANKS = 3
 SPLIT_FROM = 4
-SPLIT_CHUNKS = (5, 7, 9)
+SPLIT_CHUNKS = (4, 5, 6, 7, 8)
 HALF = T // 2
 STORE_SPLIT = 64
 

@@ -33,10 +33,11 @@ HUGE = 3.0e38
 GPSIMD_TILES = 2
 UNITS_AHEAD = 2
 TILES_AHEAD = 1
-UNIT_BANKS = 3
-SPLIT_FROM = 4
-SPLIT_CHUNKS = (4, 5, 6, 7, 8)
-HALF = T // 2
+UNIT_BANKS = 2
+PE_SUMS = 3
+SLOTS = 3
+SUMS_AT = SLOTS * P
+LAST_WIDE = N_CHUNKS - 4
 STORE_SPLIT = 64
 
 FLOPS = 2 * B * C * T * H
@@ -51,6 +52,8 @@ def tile_attentivestatspool_pb_kernel(tc, h, x, mask, w2_words, w2_scales, b2, g
         work = stack.enter_context(tc.tile_pool(name="work", bufs=2 * PER_CHUNK))
         scratch = stack.enter_context(tc.tile_pool(name="scratch", bufs=3 * GPSIMD_TILES))
         grouped = stack.enter_context(tc.tile_pool(name="grouped", bufs=1))
+        folded = stack.enter_context(tc.tile_pool(name="folded", bufs=2))
+        fold_banks = stack.enter_context(tc.psum_pool(name="fold_banks", bufs=1))
         unit_banks = stack.enter_context(tc.psum_pool(name="unit_banks", bufs=UNIT_BANKS))
         tile_banks = stack.enter_context(tc.psum_pool(name="tile_banks", bufs=PER_CHUNK))
         x_banks = stack.enter_context(tc.psum_pool(name="x_banks", bufs=1))
@@ -148,7 +151,7 @@ def tile_attentivestatspool_pb_kernel(tc, h, x, mask, w2_words, w2_scales, b2, g
                 in_=h_grouped[b][:, first:last, :].rearrange("p t j -> p (t j)"),
             )
 
-        vector_bank = unit_banks.tile([P, P], BF16, tag="logits")
+        vector_bank = fold_banks.tile([P, P], BF16, tag="logits")
         nc.tensor.transpose(vector_bank[:], vector_rows[:], identity_bf16[:])
         vectors = keep.tile([P, MASK_AT], F32)
         gain = vectors[:, 0:V_COLS]
@@ -174,7 +177,7 @@ def tile_attentivestatspool_pb_kernel(tc, h, x, mask, w2_words, w2_scales, b2, g
         regroup_h_gpsimd(2)
         last_grouped = keep.tile([P, T, PACK], BF16, align_bytes=64)
         h_grouped[3] = last_grouped
-        late_h = {1: (quantise_h, 2), SPLIT_FROM + 1: (quantise_h, 3)}
+        late_h = {1: (quantise_h, 2), 5: (quantise_h, 3)}
 
         neg_max = keep.tile([P, N_TILES], F32)
         s0 = keep.tile([P, N_TILES], F32)
@@ -188,8 +191,6 @@ def tile_attentivestatspool_pb_kernel(tc, h, x, mask, w2_words, w2_scales, b2, g
         sums_vector = keep.tile([P, 2 * B], F32)
         sums_scalar = keep.tile([P, 2 * B], F32)
         nc.gpsimd.memset(sums_scalar[:], 0.0)
-        s2_part = keep.tile([P, N_TILES], F32)
-        nc.gpsimd.memset(s2_part[:], 0.0)
         x_psum = {}
         unit_bank = {}
         unit_sb = {}
@@ -204,7 +205,8 @@ def tile_attentivestatspool_pb_kernel(tc, h, x, mask, w2_words, w2_scales, b2, g
         def unit_logits(u):
             b, rest = divmod(u, C_TILES)
             cc, tt = divmod(rest, PER_CHUNK)
-            logits = unit_banks.tile([P, C_CHUNK], F32)
+            early = u // PER_CHUNK < 2 and tt == 2
+            logits = (fold_banks if early else unit_banks).tile([P, C_CHUNK], F32, name="logits")
             nc.tensor.matmul_mx(
                 out=logits[:],
                 lhsT=h_codes[:, b, P * tt : P * (tt + 1)].bitcast(FP8X4),
@@ -286,10 +288,41 @@ def tile_attentivestatspool_pb_kernel(tc, h, x, mask, w2_words, w2_scales, b2, g
         def second_moment_sum(i):
             unused_sum = scratch.tile([P, T], BF16)
             width = weighted_sq[i].shape[1]
-            into = s2 if width == T else s2_part
             nc.scalar.activation(
                 out=unused_sum[:, 0:width], in_=weighted_sq[i], func=ACT.Copy,
-                accum_out=into[:, i : i + 1],
+                accum_out=s2[:, i : i + 1],
+            )
+
+        fold = {}
+        fold_sb = {}
+
+        def fold_products(i, slot):
+            for tt in range(PER_CHUNK):
+                nc.tensor.matmul(
+                    out=fold[0][:, P * slot : P * (slot + 1)],
+                    lhsT=weighted_sq[i][:, P * tt : P * (tt + 1)], rhs=identity[:], is_transpose=True,
+                    start=(tt == 0), stop=(tt == PER_CHUNK - 1),
+                )
+
+        def folds_to_sbuf(count):
+            fold_copy = folded.tile([P, SLOTS * P], F32)
+            nc.scalar.copy(out=fold_copy[:, 0 : P * count], in_=fold[0][:, 0 : P * count])
+            fold_sb[0] = fold_copy
+
+        def fold_sum(i, slot):
+            nc.tensor.matmul(
+                out=fold[0][:, SUMS_AT + i : SUMS_AT + i + 1],
+                lhsT=fold_sb[0][:, P * slot : P * (slot + 1)], rhs=ones[:, 0:1], start=True, stop=True,
+            )
+
+        def fold_sums_to_sbuf():
+            cols = PER_CHUNK * (LAST_WIDE + 1)
+            pick = "p (n cl) -> p n cl"
+            nc.scalar.copy(
+                out=s2[:, 0:cols].rearrange(pick, cl=PER_CHUNK)[:, :, PER_CHUNK - PE_SUMS : PER_CHUNK],
+                in_=fold[0][:, SUMS_AT : SUMS_AT + cols].rearrange(pick, cl=PER_CHUNK)[
+                    :, :, PER_CHUNK - PE_SUMS : PER_CHUNK
+                ],
             )
 
         def invert_s0():
@@ -313,59 +346,89 @@ def tile_attentivestatspool_pb_kernel(tc, h, x, mask, w2_words, w2_scales, b2, g
                 return tiles[:2]
             if n == N_CHUNKS - 2:
                 return tiles
-            if n in SPLIT_CHUNKS:
+            if n <= LAST_WIDE:
                 return [tiles[3], tiles[2], tiles[1]]
             return tiles[:1:-1]
 
         for r in range(-UNITS_AHEAD, N_CHUNKS + 1):
-            for u in members(r + UNITS_AHEAD)[:UNIT_BANKS]:
-                unit_logits(u)
-            if r == N_CHUNKS - 2:
-                for early, late in list(zip(members(r), members(r + 1)))[1:]:
-                    x_to_psum(unit_banks, [late, early])
-            for i in members(r + TILES_AHEAD):
-                tile_transposes(i)
-            if 1 <= r + 1 < N_CHUNKS - 2:
-                x_to_psum(x_banks, members(r + 1)[:1])
-            if r + 1 == N_CHUNKS - 2:
-                x_to_psum(x_banks, [members(r + 2)[0], members(r + 1)[0]])
-            for u in members(r + UNITS_AHEAD)[UNIT_BANKS:]:
-                unit_logits(u)
-            if r + 1 == 0:
-                x_to_psum(x_banks, members(r + 1)[:1])
-
             tiles = members(r)
+            following = members(r + TILES_AHEAD)
+            units_now = members(r + UNITS_AHEAD)
             sums_due = gpsimd_jobs(r - 1)
+            if r == 1:
+                fold_bank = fold_banks.tile([P, C_CHUNK], F32, tag="logits")
+                fold[0] = fold_bank
             if 0 <= r < N_CHUNKS - 2:
+                by_tensor = sums_due[:PE_SUMS]
+                by_scalar = sums_due[PE_SUMS:]
+                unit_logits(units_now[0])
+                unit_logits(units_now[1])
+                for i in by_tensor[0:1]:
+                    fold_products(i, 0)
                 for i in tiles[:3]:
                     maximum(i)
                 for i in tiles[:3]:
                     weights(i)
-                for i in sums_due[:1]:
-                    second_moment_sum(i)
+                for i in following[:3]:
+                    tile_transposes(i)
+                for i in by_tensor[1:2]:
+                    fold_products(i, 1)
+                unit_mask(units_now[0])
+                unit_logits(units_now[2])
                 first_moment(tiles[0])
                 maximum(tiles[3])
                 weights(tiles[3])
-                for i in sums_due[1:]:
+                tile_transposes(following[3])
+                unit_mask(units_now[1])
+                unit_logits(units_now[3])
+                for i in by_tensor[2:3]:
+                    fold_products(i, 2)
+                if r + 1 < N_CHUNKS - 2:
+                    x_to_psum(x_banks, following[:1])
+                else:
+                    x_to_psum(x_banks, [members(r + 2)[0], following[0]])
+                unit_mask(units_now[2])
+                unit_mask(units_now[3])
+                if by_tensor:
+                    folds_to_sbuf(len(by_tensor))
+                for slot, i in enumerate(by_tensor):
+                    fold_sum(i, slot)
+                for i in by_scalar:
                     second_moment_sum(i)
-                for u in members(r + UNITS_AHEAD):
-                    unit_mask(u)
+                if 1 <= r <= PER_CHUNK:
+                    regroup_h_scalar(3, P * (r - 1), P * r)
                 second_moment(tiles[0])
                 if r in late_h:
                     step, b = late_h[r]
                     step(b)
                 first_moment(tiles[1])
                 first_moment(tiles[2])
-                second_moment(tiles[1], HALF if r in SPLIT_CHUNKS else 0)
+                if tiles[1] not in gpsimd_jobs(r):
+                    second_moment(tiles[1])
                 first_moment(tiles[3])
-                second_moment_products(tiles[3])
-                second_moment_products(tiles[2])
-                if r < SPLIT_FROM:
-                    regroup_h_gpsimd(3, P * r, P * (r + 1))
-                if r in SPLIT_CHUNKS:
-                    second_moment_products(tiles[1], HALF)
+                for i in gpsimd_jobs(r):
+                    second_moment_products(i)
             else:
-                for u in members(r + UNITS_AHEAD):
+                for u in units_now[:3]:
+                    unit_logits(u)
+                if r == N_CHUNKS - 2:
+                    pairs = list(zip(tiles, following))[1:]
+                    for early, late in pairs[:UNIT_BANKS]:
+                        x_to_psum(unit_banks, [late, early])
+                    for i in following[:2]:
+                        tile_transposes(i)
+                    for early, late in pairs[UNIT_BANKS:]:
+                        x_to_psum(fold_banks, [late, early])
+                    for i in following[2:]:
+                        tile_transposes(i)
+                else:
+                    for i in following:
+                        tile_transposes(i)
+                for u in units_now[3:]:
+                    unit_logits(u)
+                if r + 1 == 0:
+                    x_to_psum(x_banks, following[:1])
+                for u in units_now:
                     unit_mask(u)
                 for i in tiles:
                     maximum(i)
@@ -373,7 +436,11 @@ def tile_attentivestatspool_pb_kernel(tc, h, x, mask, w2_words, w2_scales, b2, g
                     for i in sums_due[:2]:
                         second_moment_sum(i)
                     sums_due = sums_due[2:]
-                for i in tiles:
+                for i in tiles[:2]:
+                    weights(i)
+                if r == N_CHUNKS - 2:
+                    fold_sums_to_sbuf()
+                for i in tiles[2:]:
                     weights(i)
                 for i in sums_due:
                     second_moment_sum(i)
@@ -387,10 +454,6 @@ def tile_attentivestatspool_pb_kernel(tc, h, x, mask, w2_words, w2_scales, b2, g
                     step()
                     second_moment(i)
 
-        split_columns = slice(PER_CHUNK * SPLIT_FROM, PER_CHUNK * (N_CHUNKS - 2))
-        nc.vector.tensor_tensor(
-            out=s2[:, split_columns], in0=s2[:, split_columns], in1=s2_part[:, split_columns], op=ALU.add
-        )
         nc.vector.tensor_tensor(out=mean_sq[:], in0=mean, in1=mean, op=ALU.mult)
         second = keep.tile([P, B, C_TILES], F32)
         nc.vector.tensor_tensor(

@@ -34,7 +34,7 @@ GPSIMD_TILES = 2
 UNITS_AHEAD = 2
 TILES_AHEAD = 1
 UNIT_BANKS = 2
-PE_SUMS = 3
+PE_SUMS = 2
 SLOTS = 3
 SUMS_AT = SLOTS * P
 LAST_WIDE = N_CHUNKS - 4
@@ -369,30 +369,29 @@ def tile_attentivestatspool_pb_kernel(tc, h, x, mask, w2_words, w2_scales, b2, g
                     maximum(i)
                 for i in tiles[:3]:
                     weights(i)
-                for i in following[:3]:
+                for i in following[:2]:
                     tile_transposes(i)
                 for i in by_tensor[1:2]:
                     fold_products(i, 1)
+                tile_transposes(following[2])
                 unit_mask(units_now[0])
+                unit_mask(units_now[1])
                 unit_logits(units_now[2])
+                unit_logits(units_now[3])
                 first_moment(tiles[0])
                 maximum(tiles[3])
                 weights(tiles[3])
                 tile_transposes(following[3])
-                unit_mask(units_now[1])
-                unit_logits(units_now[3])
-                for i in by_tensor[2:3]:
-                    fold_products(i, 2)
                 if r + 1 < N_CHUNKS - 2:
                     x_to_psum(x_banks, following[:1])
                 else:
                     x_to_psum(x_banks, [members(r + 2)[0], following[0]])
-                unit_mask(units_now[2])
-                unit_mask(units_now[3])
                 if by_tensor:
                     folds_to_sbuf(len(by_tensor))
                 for slot, i in enumerate(by_tensor):
                     fold_sum(i, slot)
+                unit_mask(units_now[2])
+                unit_mask(units_now[3])
                 for i in by_scalar:
                     second_moment_sum(i)
                 if 1 <= r <= PER_CHUNK:

@@ -53,6 +53,7 @@ def tile_attentivestatspool_pb_kernel(tc, h, x, mask, w2_words, w2_scales, b2, g
         scratch = stack.enter_context(tc.tile_pool(name="scratch", bufs=3 * GPSIMD_TILES))
         grouped = stack.enter_context(tc.tile_pool(name="grouped", bufs=1))
         folded = stack.enter_context(tc.tile_pool(name="folded", bufs=2))
+        wide = stack.enter_context(tc.tile_pool(name="wide", bufs=2))
         fold_banks = stack.enter_context(tc.psum_pool(name="fold_banks", bufs=1))
         unit_banks = stack.enter_context(tc.psum_pool(name="unit_banks", bufs=UNIT_BANKS))
         tile_banks = stack.enter_context(tc.psum_pool(name="tile_banks", bufs=PER_CHUNK))
@@ -263,13 +264,31 @@ def tile_attentivestatspool_pb_kernel(tc, h, x, mask, w2_words, w2_scales, b2, g
         def x_for_vector(i):
             return x_psum.get(i, x_tile(i))
 
+        wide_y = {}
+
         def first_moment(i):
-            y = work.tile([P, T], F32)
+            n, cl = divmod(i, PER_CHUNK)
+            if n < N_CHUNKS - 2 and cl > 0:
+                if n not in wide_y:
+                    y_wide = wide.tile([P, PER_CHUNK - 1, T], F32)
+                    wide_y[n] = y_wide
+                weighted[i] = wide_y[n][:, cl - 1, :]
+            else:
+                y = work.tile([P, T], F32)
+                weighted[i] = y[:]
             nc.vector.scalar_tensor_tensor(
-                out=y[:], in0=weight[i][:], scalar=1.0, in1=x_for_vector(i), op0=ALU.mult, op1=ALU.mult,
-                accum_out=s1[:, i : i + 1],
+                out=weighted[i], in0=weight[i][:], scalar=1.0, in1=x_for_vector(i), op0=ALU.mult,
+                op1=ALU.mult, accum_out=s1[:, i : i + 1],
             )
-            weighted[i] = y
+
+        def second_moment_products_wide(n, first):
+            y2_wide = wide.tile([P, PER_CHUNK - 1, T], F32)
+            nc.gpsimd.tensor_tensor(
+                out=y2_wide[:, first - 1 : PER_CHUNK - 1, :], in0=wide_y[n][:, first - 1 : PER_CHUNK - 1, :],
+                in1=x_sb[n][:, first:PER_CHUNK, :], op=ALU.mult,
+            )
+            for cl in range(first, PER_CHUNK):
+                weighted_sq[PER_CHUNK * n + cl] = y2_wide[:, cl - 1, :]
 
         def second_moment(i, first=0):
             unused = scratch.tile([P, T], BF16)
@@ -363,17 +382,12 @@ def tile_attentivestatspool_pb_kernel(tc, h, x, mask, w2_words, w2_scales, b2, g
                 by_scalar = sums_due[PE_SUMS:]
                 unit_logits(units_now[0])
                 unit_logits(units_now[1])
-                for i in by_tensor[0:1]:
-                    fold_products(i, 0)
                 for i in tiles[:3]:
                     maximum(i)
                 for i in tiles[:3]:
                     weights(i)
-                for i in following[:2]:
+                for i in following[:3]:
                     tile_transposes(i)
-                for i in by_tensor[1:2]:
-                    fold_products(i, 1)
-                tile_transposes(following[2])
                 unit_mask(units_now[0])
                 unit_mask(units_now[1])
                 unit_logits(units_now[2])
@@ -381,19 +395,21 @@ def tile_attentivestatspool_pb_kernel(tc, h, x, mask, w2_words, w2_scales, b2, g
                 first_moment(tiles[0])
                 maximum(tiles[3])
                 weights(tiles[3])
+                for slot, i in enumerate(by_tensor):
+                    fold_products(i, slot)
                 tile_transposes(following[3])
                 if r + 1 < N_CHUNKS - 2:
                     x_to_psum(x_banks, following[:1])
                 else:
                     x_to_psum(x_banks, [members(r + 2)[0], following[0]])
-                if by_tensor:
-                    folds_to_sbuf(len(by_tensor))
-                for slot, i in enumerate(by_tensor):
-                    fold_sum(i, slot)
                 unit_mask(units_now[2])
                 unit_mask(units_now[3])
                 for i in by_scalar:
                     second_moment_sum(i)
+                if by_tensor:
+                    folds_to_sbuf(len(by_tensor))
+                for slot, i in enumerate(by_tensor):
+                    fold_sum(i, slot)
                 if 1 <= r <= PER_CHUNK:
                     regroup_h_scalar(3, P * (r - 1), P * r)
                 second_moment(tiles[0])
@@ -405,8 +421,7 @@ def tile_attentivestatspool_pb_kernel(tc, h, x, mask, w2_words, w2_scales, b2, g
                 if tiles[1] not in gpsimd_jobs(r):
                     second_moment(tiles[1])
                 first_moment(tiles[3])
-                for i in gpsimd_jobs(r):
-                    second_moment_products(i)
+                second_moment_products_wide(r, PER_CHUNK - len(gpsimd_jobs(r)))
             else:
                 for u in units_now[:3]:
                     unit_logits(u)

@@ -369,17 +369,23 @@ def tile_attentivestatspool_pb_kernel(tc, h, x, mask, w2_words, w2_scales, b2, g
                 return [tiles[3], tiles[2], tiles[1]]
             return tiles[:1:-1]
 
+        def tensor_sums(n):
+            return gpsimd_jobs(n)[:PE_SUMS] if 0 <= n <= LAST_WIDE else []
+
+        def scalar_sums(n):
+            return gpsimd_jobs(n)[len(tensor_sums(n)) :]
+
         for r in range(-UNITS_AHEAD, N_CHUNKS + 1):
             tiles = members(r)
             following = members(r + TILES_AHEAD)
             units_now = members(r + UNITS_AHEAD)
-            sums_due = gpsimd_jobs(r - 1)
+            sums_due = scalar_sums(r - 1)
+            to_fold = tensor_sums(r - 1)
+            to_sum = tensor_sums(r - 2)
             if r == 1:
                 fold_bank = fold_banks.tile([P, C_CHUNK], F32, tag="logits")
                 fold[0] = fold_bank
             if 0 <= r < N_CHUNKS - 2:
-                by_tensor = sums_due[:PE_SUMS]
-                by_scalar = sums_due[PE_SUMS:]
                 unit_logits(units_now[0])
                 unit_logits(units_now[1])
                 for i in tiles[:3]:
@@ -388,6 +394,10 @@ def tile_attentivestatspool_pb_kernel(tc, h, x, mask, w2_words, w2_scales, b2, g
                     weights(i)
                 for i in following[:3]:
                     tile_transposes(i)
+                if to_sum:
+                    folds_to_sbuf(len(to_sum))
+                for slot, i in enumerate(to_sum):
+                    fold_sum(i, slot)
                 unit_mask(units_now[0])
                 unit_mask(units_now[1])
                 unit_logits(units_now[2])
@@ -395,21 +405,17 @@ def tile_attentivestatspool_pb_kernel(tc, h, x, mask, w2_words, w2_scales, b2, g
                 first_moment(tiles[0])
                 maximum(tiles[3])
                 weights(tiles[3])
-                for slot, i in enumerate(by_tensor):
-                    fold_products(i, slot)
                 tile_transposes(following[3])
                 if r + 1 < N_CHUNKS - 2:
                     x_to_psum(x_banks, following[:1])
                 else:
                     x_to_psum(x_banks, [members(r + 2)[0], following[0]])
+                for slot, i in enumerate(to_fold):
+                    fold_products(i, slot)
                 unit_mask(units_now[2])
                 unit_mask(units_now[3])
-                for i in by_scalar:
+                for i in sums_due:
                     second_moment_sum(i)
-                if by_tensor:
-                    folds_to_sbuf(len(by_tensor))
-                for slot, i in enumerate(by_tensor):
-                    fold_sum(i, slot)
                 if 1 <= r <= PER_CHUNK:
                     regroup_h_scalar(3, P * (r - 1), P * r)
                 second_moment(tiles[0])
@@ -431,6 +437,13 @@ def tile_attentivestatspool_pb_kernel(tc, h, x, mask, w2_words, w2_scales, b2, g
                         x_to_psum(unit_banks, [late, early])
                     for i in following[:2]:
                         tile_transposes(i)
+                    for i in tiles[:2]:
+                        maximum(i)
+                    for i in tiles[:2]:
+                        weights(i)
+                    folds_to_sbuf(len(to_sum))
+                    for slot, i in enumerate(to_sum):
+                        fold_sum(i, slot)
                     for early, late in pairs[UNIT_BANKS:]:
                         x_to_psum(fold_banks, [late, early])
                     for i in following[2:]:
@@ -444,18 +457,16 @@ def tile_attentivestatspool_pb_kernel(tc, h, x, mask, w2_words, w2_scales, b2, g
                     x_to_psum(x_banks, following[:1])
                 for u in units_now:
                     unit_mask(u)
-                for i in tiles:
+                for i in tiles[2:] if r == N_CHUNKS - 2 else tiles:
                     maximum(i)
                 if r == N_CHUNKS - 1:
                     for i in sums_due[:2]:
                         second_moment_sum(i)
                     sums_due = sums_due[2:]
-                for i in tiles[:2]:
+                for i in tiles[2:] if r == N_CHUNKS - 2 else tiles:
                     weights(i)
                 if r == N_CHUNKS - 2:
                     fold_sums_to_sbuf()
-                for i in tiles[2:]:
-                    weights(i)
                 for i in sums_due:
                     second_moment_sum(i)
                 for i in gpsimd_jobs(r):

@@ -396,8 +396,6 @@ def tile_attentivestatspool_pb_kernel(tc, h, x, mask, w2_words, w2_scales, b2, g
                     tile_transposes(i)
                 if to_sum:
                     folds_to_sbuf(len(to_sum))
-                for slot, i in enumerate(to_sum):
-                    fold_sum(i, slot)
                 unit_mask(units_now[0])
                 unit_mask(units_now[1])
                 unit_logits(units_now[2])
@@ -410,14 +408,16 @@ def tile_attentivestatspool_pb_kernel(tc, h, x, mask, w2_words, w2_scales, b2, g
                     x_to_psum(x_banks, following[:1])
                 else:
                     x_to_psum(x_banks, [members(r + 2)[0], following[0]])
+                for slot, i in enumerate(to_sum):
+                    fold_sum(i, slot)
                 for slot, i in enumerate(to_fold):
                     fold_products(i, slot)
-                unit_mask(units_now[2])
-                unit_mask(units_now[3])
                 for i in sums_due:
                     second_moment_sum(i)
                 if 1 <= r <= PER_CHUNK:
                     regroup_h_scalar(3, P * (r - 1), P * r)
+                unit_mask(units_now[2])
+                unit_mask(units_now[3])
                 second_moment(tiles[0])
                 if r in late_h:
                     step, b = late_h[r]

@@ -414,14 +414,14 @@ def tile_attentivestatspool_pb_kernel(tc, h, x, mask, w2_words, w2_scales, b2, g
                     fold_products(i, slot)
                 for i in sums_due:
                     second_moment_sum(i)
-                if 1 <= r <= PER_CHUNK:
-                    regroup_h_scalar(3, P * (r - 1), P * r)
                 unit_mask(units_now[2])
                 unit_mask(units_now[3])
                 second_moment(tiles[0])
                 if r in late_h:
                     step, b = late_h[r]
                     step(b)
+                if 1 <= r <= PER_CHUNK:
+                    regroup_h(3, P * (r - 1), P * r)
                 first_moment(tiles[1])
                 first_moment(tiles[2])
                 if tiles[1] not in gpsimd_jobs(r):

@@ -175,9 +175,11 @@ def tile_attentivestatspool_pb_kernel(tc, h, x, mask, w2_words, w2_scales, b2, g
         regroup_h(1)
         quantise_h(1)
         next_grouped(2)
-        regroup_h_gpsimd(2)
+        regroup_h(2)
         last_grouped = keep.tile([P, T, PACK], BF16, align_bytes=64)
         h_grouped[3] = last_grouped
+        for tt in range(PER_CHUNK):
+            regroup_h_gpsimd(3, P * tt, P * (tt + 1))
         late_h = {1: (quantise_h, 2), 5: (quantise_h, 3)}
 
         neg_max = keep.tile([P, N_TILES], F32)
@@ -420,8 +422,6 @@ def tile_attentivestatspool_pb_kernel(tc, h, x, mask, w2_words, w2_scales, b2, g
                 if r in late_h:
                     step, b = late_h[r]
                     step(b)
-                if 1 <= r <= PER_CHUNK:
-                    regroup_h(3, P * (r - 1), P * r)
                 first_moment(tiles[1])
                 first_moment(tiles[2])
                 if tiles[1] not in gpsimd_jobs(r):

@@ -51,7 +51,7 @@ def tile_attentivestatspool_pb_kernel(tc, h, x, mask, w2_words, w2_scales, b2, g
         units = stack.enter_context(tc.tile_pool(name="units", bufs=2 * PER_CHUNK))
         work = stack.enter_context(tc.tile_pool(name="work", bufs=2 * PER_CHUNK))
         scratch = stack.enter_context(tc.tile_pool(name="scratch", bufs=3 * GPSIMD_TILES))
-        grouped = stack.enter_context(tc.tile_pool(name="grouped", bufs=1))
+        grouped = stack.enter_context(tc.tile_pool(name="grouped", bufs=2))
         folded = stack.enter_context(tc.tile_pool(name="folded", bufs=2))
         wide = stack.enter_context(tc.tile_pool(name="wide", bufs=2))
         fold_banks = stack.enter_context(tc.psum_pool(name="fold_banks", bufs=1))
@@ -173,14 +173,15 @@ def tile_attentivestatspool_pb_kernel(tc, h, x, mask, w2_words, w2_scales, b2, g
             quantise_h(0, P * tt, P * (tt + 1))
         next_grouped(1)
         regroup_h(1)
-        quantise_h(1)
         next_grouped(2)
         regroup_h(2)
+        quantise_h(1)
+        quantise_h(2)
         last_grouped = keep.tile([P, T, PACK], BF16, align_bytes=64)
         h_grouped[3] = last_grouped
         for tt in range(PER_CHUNK):
             regroup_h_gpsimd(3, P * tt, P * (tt + 1))
-        late_h = {1: (quantise_h, 2), 5: (quantise_h, 3)}
+        late_h = {5: (quantise_h, 3)}
 
         neg_max = keep.tile([P, N_TILES], F32)
         s0 = keep.tile([P, N_TILES], F32)
@@ -367,9 +368,7 @@ def tile_attentivestatspool_pb_kernel(tc, h, x, mask, w2_words, w2_scales, b2, g
                 return tiles[:2]
             if n == N_CHUNKS - 2:
                 return tiles
-            if n <= LAST_WIDE:
-                return [tiles[3], tiles[2], tiles[1]]
-            return tiles[:1:-1]
+            return [tiles[3], tiles[2], tiles[1]]
 
         def tensor_sums(n):
             return gpsimd_jobs(n)[:PE_SUMS] if 0 <= n <= LAST_WIDE else []

from contextlib import ExitStack

import concourse.mybir as mybir
from concourse.masks import make_identity

F32 = mybir.dt.float32
BF16 = mybir.dt.bfloat16
I32 = mybir.dt.int32
U32 = mybir.dt.uint32
U8 = mybir.dt.uint8
FP8X4 = mybir.dt.float8_e4m3fn_x4
FP4X4 = mybir.dt.float4_e2m1fn_x4
ALU = mybir.AluOpType
ACT = mybir.ActivationFunctionType
AX = mybir.AxisListType

B, C, T, H = 4, 1536, 512, 512
EPS_LN = 1e-5
EPS_STD = 1e-5
P = 128
PACK = 4
QUADRANT = 32
C_TILES = C // P
N_TILES = B * C_TILES
C_CHUNK = 512
PER_CHUNK = T // P
N_CHUNKS = N_TILES // PER_CHUNK
X_GROUP = PER_CHUNK
V_COLS = 2 * C_TILES
MASK_AT = 2 * V_COLS
MASK_COLS = B * PER_CHUNK
HUGE = 3.0e38
GPSIMD_TILES = 2
UNITS_AHEAD = 2
TILES_AHEAD = 1
UNIT_BANKS = 2
PE_SUMS = 2
SLOTS = 3
SUMS_AT = SLOTS * P
LAST_WIDE = N_CHUNKS - 4
STORE_SPLIT = 64

FLOPS = 2 * B * C * T * H


def tile_attentivestatspool_pb_kernel(tc, h, x, mask, w2_words, w2_scales, b2, g2, be2, out):
    nc = tc.nc
    with ExitStack() as stack:
        stack.enter_context(tc.manual_schedule())
        keep = stack.enter_context(tc.tile_pool(name="keep", bufs=1))
        units = stack.enter_context(tc.tile_pool(name="units", bufs=2 * PER_CHUNK))
        work = stack.enter_context(tc.tile_pool(name="work", bufs=2 * PER_CHUNK))
        scratch = stack.enter_context(tc.tile_pool(name="scratch", bufs=3 * GPSIMD_TILES))
        grouped = stack.enter_context(tc.tile_pool(name="grouped", bufs=2))
        folded = stack.enter_context(tc.tile_pool(name="folded", bufs=2))
        wide = stack.enter_context(tc.tile_pool(name="wide", bufs=2))
        fold_banks = stack.enter_context(tc.psum_pool(name="fold_banks", bufs=1))
        unit_banks = stack.enter_context(tc.psum_pool(name="unit_banks", bufs=UNIT_BANKS))
        tile_banks = stack.enter_context(tc.psum_pool(name="tile_banks", bufs=PER_CHUNK))
        x_banks = stack.enter_context(tc.psum_pool(name="x_banks", bufs=1))

        h_raw = []
        for b in range(B):
            h_raw.append(keep.tile([P, PACK, T], BF16, name="h_raw_%d" % b))
        x_sb = []
        for i in range(N_TILES // X_GROUP):
            x_sb.append(keep.tile([P, X_GROUP, T], BF16, name="x_sb_%d" % i))
        w_words = keep.tile([P, 2 * C], U8, align_bytes=64)
        w_planes = keep.tile([P, C], U8, align_bytes=64)
        nc.vector.memset(w_planes[:].bitcast(I32), 0)

        def load_h(b, first=0, last=T):
            rows = h[b].rearrange("(p j) t -> p j t", j=PACK)
            nc.sync.dma_start(out=h_raw[b][:, :, first:last], in_=rows[:, :, first:last])

        def load_words(first, last):
            nc.sync.dma_start(
                out=w_words[:, first:last].bitcast(I32),
                in_=w2_words.rearrange("g p n -> (g p) n")[:, first:last].bitcast(I32),
            )

        def load_x(i):
            b, first = divmod(i * X_GROUP, C_TILES)
            rows = x[b].rearrange("(ct p) t -> p ct t", p=P)
            nc.sync.dma_start(out=x_sb[i][:], in_=rows[:, first : first + X_GROUP, :])

        load_h(0)
        load_words(0, 2 * C)
        for quadrant in range(P // QUADRANT):
            nc.sync.dma_start(
                out=w_planes[QUADRANT * quadrant : QUADRANT * quadrant + PACK, :].bitcast(I32),
                in_=w2_scales[0, PACK * quadrant : PACK * (quadrant + 1), :].bitcast(I32),
            )
        load_h(1)
        load_h(2)
        load_x(0)
        load_h(3)
        for i in range(1, N_TILES // X_GROUP):
            load_x(i)

        vector_rows = keep.tile([P, P], BF16)
        nc.gpsimd.memset(vector_rows[MASK_AT + MASK_COLS : P, :], 0.0)
        nc.scalar.dma_start(
            out=vector_rows[MASK_AT : MASK_AT + MASK_COLS, :],
            in_=mask.rearrange("b o (tt p) -> (b o tt) p", p=P),
        )
        nc.scalar.dma_start(out=vector_rows[0:V_COLS, :], in_=g2.rearrange("(j p) -> j p", p=P))
        nc.scalar.dma_start(
            out=vector_rows[V_COLS : 2 * V_COLS, :], in_=be2.rearrange("(j p) -> j p", p=P)
        )

        identity_bf16 = keep.tile([P, P], BF16)
        make_identity(nc, identity_bf16[:])
        identity = keep.tile([P, P], F32)
        make_identity(nc, identity[:])
        ones = keep.tile([P, P], F32)
        nc.gpsimd.memset(ones[:], 1.0)
        result = keep.tile([P, P], F32)
        nc.gpsimd.memset(result[:], 0.0)

        h_codes = keep.tile([P, B, T], U32, align_bytes=64)
        h_planes = keep.tile([P, B, T], U8, align_bytes=64)
        first_grouped = keep.tile([P, T, PACK], BF16, align_bytes=64)
        h_grouped = {0: first_grouped}

        def next_grouped(b):
            later_grouped = grouped.tile([P, T, PACK], BF16, align_bytes=64)
            h_grouped[b] = later_grouped

        def regroup_h_gpsimd(b, first=0, last=T):
            nc.gpsimd.tensor_scalar(
                out=h_grouped[b][:, first:last, :],
                in0=h_raw[b][:, :, first:last].rearrange("p j t -> p t j"), scalar1=1.0,
                scalar2=0.0, op0=ALU.mult, op1=ALU.add,
            )

        def regroup_h_scalar(b, first, last):
            nc.scalar.copy(
                out=h_grouped[b][:, first:last, :], in_=h_raw[b][:, :, first:last].rearrange("p j t -> p t j")
            )

        def regroup_h(b, first=0, last=T):
            nc.vector.tensor_copy(
                out=h_grouped[b][:, first:last, :].rearrange("p (c i) j -> p c j i", i=4),
                in_=h_raw[b][:, :, first:last].rearrange("p j (c i) -> p c j i", i=4),
            )

        def quantise_h(b, first=0, last=T):
            nc.vector.quantize_mx(
                out=h_codes[:, b, first:last].bitcast(FP8X4),
                scales=h_planes[:, b, first:last],
                in_=h_grouped[b][:, first:last, :].rearrange("p t j -> p (t j)"),
            )

        vector_bank = fold_banks.tile([P, P], BF16, tag="logits")
        nc.tensor.transpose(vector_bank[:], vector_rows[:], identity_bf16[:])
        vectors = keep.tile([P, MASK_AT], F32)
        gain = vectors[:, 0:V_COLS]
        bias = vectors[:, V_COLS : 2 * V_COLS]
        mask_bias = keep.tile([P, MASK_COLS], F32)

        regroup_h(0, 0, P)
        regroup_h(0, P, 2 * P)
        quantise_h(0, 0, P)
        nc.vector.tensor_scalar(
            out=mask_bias[:], in0=vector_bank[:, MASK_AT : MASK_AT + MASK_COLS], scalar1=1.0,
            scalar2=HUGE, op0=ALU.subtract, op1=ALU.mult,
        )
        for tt in range(2, PER_CHUNK):
            regroup_h_scalar(0, P * tt, P * (tt + 1))
        nc.scalar.copy(out=vectors[:], in_=vector_bank[:, 0:MASK_AT])
        for tt in range(1, PER_CHUNK):
            quantise_h(0, P * tt, P * (tt + 1))
        next_grouped(1)
        regroup_h(1)
        next_grouped(2)
        regroup_h(2)
        quantise_h(1)
        quantise_h(2)
        last_grouped = keep.tile([P, T, PACK], BF16, align_bytes=64)
        h_grouped[3] = last_grouped
        for tt in range(PER_CHUNK):
            regroup_h_gpsimd(3, P * tt, P * (tt + 1))
        late_h = {5: (quantise_h, 3)}

        neg_max = keep.tile([P, N_TILES], F32)
        s0 = keep.tile([P, N_TILES], F32)
        s1 = keep.tile([P, N_TILES], F32)
        s2 = keep.tile([P, N_TILES], F32)
        by_b = "p (b c) -> p b c"
        inv_s0 = keep.tile([P, N_TILES], F32)
        pooled = keep.tile([P, B, 2, C_TILES], F32)
        mean = pooled[:, :, 0, :]
        mean_sq = keep.tile([P, B, C_TILES], F32)
        sums_vector = keep.tile([P, 2 * B], F32)
        sums_scalar = keep.tile([P, 2 * B], F32)
        nc.gpsimd.memset(sums_scalar[:], 0.0)
        x_psum = {}
        unit_bank = {}
        unit_sb = {}
        masked = {}
        weight = {}
        weighted = {}
        weighted_sq = {}

        def x_tile(i):
            return x_sb[i // X_GROUP][:, i % X_GROUP, :]

        def unit_logits(u):
            b, rest = divmod(u, C_TILES)
            cc, tt = divmod(rest, PER_CHUNK)
            early = u // PER_CHUNK < 2 and tt == 2
            logits = (fold_banks if early else unit_banks).tile([P, C_CHUNK], F32, name="logits")
            nc.tensor.matmul_mx(
                out=logits[:],
                lhsT=h_codes[:, b, P * tt : P * (tt + 1)].bitcast(FP8X4),
                lhsT_scale=h_planes[:, b, P * tt : P * (tt + 1)],
                rhs=w_words[:, 2 * C_CHUNK * cc : 2 * C_CHUNK * (cc + 1)].bitcast(FP4X4),
                rhs_scale=w_planes[:, C_CHUNK * cc : C_CHUNK * (cc + 1)],
                start=True,
                stop=True,
            )
            unit_bank[u] = logits

        def unit_mask(u):
            column = PER_CHUNK * (u // C_TILES) + u % PER_CHUNK
            am_t = units.tile([P, C_CHUNK], F32)
            nc.scalar.activation(
                out=am_t[:], in_=unit_bank[u][:], func=ACT.Identity,
                bias=mask_bias[:, column : column + 1], scale=1.0,
            )
            unit_sb[u] = am_t

        def tile_transposes(i):
            first_unit = PER_CHUNK * (i // PER_CHUNK)
            cl = i % PER_CHUNK
            am = tile_banks.tile([P, T], F32)
            for tt in range(PER_CHUNK):
                nc.tensor.transpose(
                    am[:, P * tt : P * (tt + 1)],
                    unit_sb[first_unit + tt][:, P * cl : P * (cl + 1)],
                    identity[:],
                )
            masked[i] = am

        def maximum(i):
            nc.vector.tensor_reduce(
                out=neg_max[:, i : i + 1], in_=masked[i][:], axis=AX.X, op=ALU.max, negate=True
            )

        def weights(i):
            e = work.tile([P, T], F32)
            nc.scalar.activation(
                out=e[:], in_=masked[i][:], func=ACT.Exp, bias=neg_max[:, i : i + 1], scale=1.0,
                accum_out=s0[:, i : i + 1],
            )
            weight[i] = e

        def x_to_psum(pool, tiles):
            bank = pool.tile([P, 2, T], BF16, tag="logits")
            for half, i in enumerate(tiles):
                nc.tensor.matmul(
                    out=bank[:, half, :], lhsT=identity_bf16[:], rhs=x_tile(i), start=True, stop=True
                )
                x_psum[i] = bank[:, half, :]

        def x_for_vector(i):
            return x_psum.get(i, x_tile(i))

        wide_y = {}

        def first_moment(i):
            n, cl = divmod(i, PER_CHUNK)
            if n < N_CHUNKS - 2 and cl > 0:
                if n not in wide_y:
                    y_wide = wide.tile([P, PER_CHUNK - 1, T], F32)
                    wide_y[n] = y_wide
                weighted[i] = wide_y[n][:, cl - 1, :]
            else:
                y = work.tile([P, T], F32)
                weighted[i] = y[:]
            nc.vector.scalar_tensor_tensor(
                out=weighted[i], in0=weight[i][:], scalar=1.0, in1=x_for_vector(i), op0=ALU.mult,
                op1=ALU.mult, accum_out=s1[:, i : i + 1],
            )

        def second_moment_products_wide(n, first):
            y2_wide = wide.tile([P, PER_CHUNK - 1, T], F32)
            nc.gpsimd.tensor_tensor(
                out=y2_wide[:, first - 1 : PER_CHUNK - 1, :], in0=wide_y[n][:, first - 1 : PER_CHUNK - 1, :],
                in1=x_sb[n][:, first:PER_CHUNK, :], op=ALU.mult,
            )
            for cl in range(first, PER_CHUNK):
                weighted_sq[PER_CHUNK * n + cl] = y2_wide[:, cl - 1, :]

        def second_moment(i, first=0):
            unused = scratch.tile([P, T], BF16)
            nc.vector.scalar_tensor_tensor(
                out=unused[:, first:T], in0=weighted[i][:, first:T], scalar=1.0,
                in1=x_for_vector(i)[:, first:T], op0=ALU.mult, op1=ALU.mult, accum_out=s2[:, i : i + 1],
            )

        def second_moment_products(i, last=T):
            y2 = scratch.tile([P, T], F32)
            nc.gpsimd.tensor_tensor(
                out=y2[:, 0:last], in0=weighted[i][:, 0:last], in1=x_tile(i)[:, 0:last], op=ALU.mult
            )
            weighted_sq[i] = y2[:, 0:last]

        def second_moment_sum(i):
            unused_sum = scratch.tile([P, T], BF16)
            width = weighted_sq[i].shape[1]
            nc.scalar.activation(
                out=unused_sum[:, 0:width], in_=weighted_sq[i], func=ACT.Copy,
                accum_out=s2[:, i : i + 1],
            )

        fold = {}
        fold_sb = {}

        def fold_products(i, slot):
            for tt in range(PER_CHUNK):
                nc.tensor.matmul(
                    out=fold[0][:, P * slot : P * (slot + 1)],
                    lhsT=weighted_sq[i][:, P * tt : P * (tt + 1)], rhs=identity[:], is_transpose=True,
                    start=(tt == 0), stop=(tt == PER_CHUNK - 1),
                )

        def folds_to_sbuf(count):
            fold_copy = folded.tile([P, SLOTS * P], F32)
            nc.scalar.copy(out=fold_copy[:, 0 : P * count], in_=fold[0][:, 0 : P * count])
            fold_sb[0] = fold_copy

        def fold_sum(i, slot):
            nc.tensor.matmul(
                out=fold[0][:, SUMS_AT + i : SUMS_AT + i + 1],
                lhsT=fold_sb[0][:, P * slot : P * (slot + 1)], rhs=ones[:, 0:1], start=True, stop=True,
            )

        def fold_sums_to_sbuf():
            cols = PER_CHUNK * (LAST_WIDE + 1)
            pick = "p (n cl) -> p n cl"
            nc.scalar.copy(
                out=s2[:, 0:cols].rearrange(pick, cl=PER_CHUNK)[:, :, PER_CHUNK - PE_SUMS : PER_CHUNK],
                in_=fold[0][:, SUMS_AT : SUMS_AT + cols].rearrange(pick, cl=PER_CHUNK)[
                    :, :, PER_CHUNK - PE_SUMS : PER_CHUNK
                ],
            )

        def invert_s0():
            nc.vector.reciprocal(out=inv_s0[:], in_=s0[:])

        def means():
            nc.vector.tensor_tensor(
                out=mean, in0=s1[:].rearrange(by_b, b=B), in1=inv_s0[:].rearrange(by_b, b=B), op=ALU.mult
            )

        def members(n):
            if 0 <= n < N_CHUNKS:
                return list(range(PER_CHUNK * n, PER_CHUNK * (n + 1)))
            return []

        def gpsimd_jobs(n):
            tiles = members(n)
            if not tiles:
                return []
            if n == N_CHUNKS - 1:
                return tiles[:2]
            if n == N_CHUNKS - 2:
                return tiles
            return [tiles[3], tiles[2], tiles[1]]

        def tensor_sums(n):
            return gpsimd_jobs(n)[:PE_SUMS] if 0 <= n <= LAST_WIDE else []

        def scalar_sums(n):
            return gpsimd_jobs(n)[len(tensor_sums(n)) :]

        for r in range(-UNITS_AHEAD, N_CHUNKS + 1):
            tiles = members(r)
            following = members(r + TILES_AHEAD)
            units_now = members(r + UNITS_AHEAD)
            sums_due = scalar_sums(r - 1)
            to_fold = tensor_sums(r - 1)
            to_sum = tensor_sums(r - 2)
            if r == 1:
                fold_bank = fold_banks.tile([P, C_CHUNK], F32, tag="logits")
                fold[0] = fold_bank
            if 0 <= r < N_CHUNKS - 2:
                unit_logits(units_now[0])
                unit_logits(units_now[1])
                for i in tiles[:3]:
                    maximum(i)
                for i in tiles[:3]:
                    weights(i)
                for i in following[:3]:
                    tile_transposes(i)
                if to_sum:
                    folds_to_sbuf(len(to_sum))
                unit_mask(units_now[0])
                unit_mask(units_now[1])
                unit_logits(units_now[2])
                unit_logits(units_now[3])
                first_moment(tiles[0])
                maximum(tiles[3])
                weights(tiles[3])
                tile_transposes(following[3])
                if r + 1 < N_CHUNKS - 2:
                    x_to_psum(x_banks, following[:1])
                else:
                    x_to_psum(x_banks, [members(r + 2)[0], following[0]])
                for slot, i in enumerate(to_sum):
                    fold_sum(i, slot)
                for slot, i in enumerate(to_fold):
                    fold_products(i, slot)
                for i in sums_due:
                    second_moment_sum(i)
                unit_mask(units_now[2])
                unit_mask(units_now[3])
                second_moment(tiles[0])
                if r in late_h:
                    step, b = late_h[r]
                    step(b)
                first_moment(tiles[1])
                first_moment(tiles[2])
                if tiles[1] not in gpsimd_jobs(r):
                    second_moment(tiles[1])
                first_moment(tiles[3])
                second_moment_products_wide(r, PER_CHUNK - len(gpsimd_jobs(r)))
            else:
                for u in units_now[:3]:
                    unit_logits(u)
                if r == N_CHUNKS - 2:
                    pairs = list(zip(tiles, following))[1:]
                    for early, late in pairs[:UNIT_BANKS]:
                        x_to_psum(unit_banks, [late, early])
                    for i in following[:2]:
                        tile_transposes(i)
                    for i in tiles[:2]:
                        maximum(i)
                    for i in tiles[:2]:
                        weights(i)
                    folds_to_sbuf(len(to_sum))
                    for slot, i in enumerate(to_sum):
                        fold_sum(i, slot)
                    for early, late in pairs[UNIT_BANKS:]:
                        x_to_psum(fold_banks, [late, early])
                    for i in following[2:]:
                        tile_transposes(i)
                else:
                    for i in following:
                        tile_transposes(i)
                for u in units_now[3:]:
                    unit_logits(u)
                if r + 1 == 0:
                    x_to_psum(x_banks, following[:1])
                for u in units_now:
                    unit_mask(u)
                for i in tiles[2:] if r == N_CHUNKS - 2 else tiles:
                    maximum(i)
                if r == N_CHUNKS - 1:
                    for i in sums_due[:2]:
                        second_moment_sum(i)
                    sums_due = sums_due[2:]
                for i in tiles[2:] if r == N_CHUNKS - 2 else tiles:
                    weights(i)
                if r == N_CHUNKS - 2:
                    fold_sums_to_sbuf()
                for i in sums_due:
                    second_moment_sum(i)
                for i in gpsimd_jobs(r):
                    first_moment(i)
                    second_moment_products(i)
                own = [i for i in tiles if i not in gpsimd_jobs(r)]
                for i in own:
                    first_moment(i)
                for step, i in zip([invert_s0, means], own):
                    step()
                    second_moment(i)

        nc.vector.tensor_tensor(out=mean_sq[:], in0=mean, in1=mean, op=ALU.mult)
        second = keep.tile([P, B, C_TILES], F32)
        nc.vector.tensor_tensor(
            out=second[:], in0=s2[:].rearrange(by_b, b=B), in1=inv_s0[:].rearrange(by_b, b=B), op=ALU.mult
        )
        mean_sq_floor = keep.tile([P, B, C_TILES], F32)
        nc.vector.tensor_scalar_add(out=mean_sq_floor[:], in0=mean_sq[:], scalar1=EPS_STD)
        var = keep.tile([P, B, C_TILES], F32)
        nc.vector.tensor_tensor(out=var[:], in0=second[:], in1=mean_sq[:], op=ALU.subtract)
        squares = keep.tile([P, B, C_TILES], F32)
        nc.vector.tensor_tensor(out=squares[:], in0=second[:], in1=mean_sq_floor[:], op=ALU.max)
        var_floor = keep.tile([P, B, C_TILES], F32)
        nc.vector.tensor_scalar_max(out=var_floor[:], in0=var[:], scalar1=EPS_STD)
        for b in range(B):
            nc.scalar.activation(
                out=pooled[:, b, 1, :], in_=var_floor[:, b, :], func=ACT.Sqrt,
                accum_out=sums_scalar[:, b : b + 1],
            )

        nc.vector.tensor_reduce(out=sums_vector[:, B : 2 * B], in_=squares[:], axis=AX.X, op=ALU.add)
        nc.vector.tensor_reduce(out=sums_vector[:, 0:B], in_=mean, axis=AX.X, op=ALU.add)
        totals = unit_banks.tile([P, 2 * B], F32, tag="logits")
        nc.tensor.matmul(out=totals[:], lhsT=ones[:], rhs=sums_vector[:], start=True, stop=False)
        nc.tensor.matmul(out=totals[:], lhsT=ones[:], rhs=sums_scalar[:], start=False, stop=True)
        moments = keep.tile([P, 2 * B], F32)
        nc.vector.tensor_scalar_mul(out=moments[:], in0=totals[:], scalar1=1.0 / (2 * C))
        mu = moments[:, 0:B]
        wide = [P, B, V_COLS]
        mu_sq = keep.tile([P, B], F32)
        nc.vector.tensor_tensor(out=mu_sq[:], in0=mu, in1=mu, op=ALU.mult)
        pooled_rows = pooled[:].rearrange("p b s c -> p b (s c)")
        centred = keep.tile(wide, F32)
        nc.vector.tensor_tensor(
            out=centred[:], in0=pooled_rows, in1=mu.unsqueeze(2).to_broadcast(wide), op=ALU.subtract
        )
        ln_var = keep.tile([P, B], F32)
        nc.vector.scalar_tensor_tensor(
            out=ln_var[:], in0=moments[:, B : 2 * B], scalar=EPS_LN, in1=mu_sq[:],
            op0=ALU.add, op1=ALU.subtract,
        )
        ln_std = keep.tile([P, B], F32)
        nc.scalar.activation(out=ln_std[:], in_=ln_var[:], func=ACT.Sqrt)
        gained = keep.tile(wide, F32)
        nc.vector.tensor_tensor(
            out=gained[:], in0=centred[:],
            in1=gain.unsqueeze(1).to_broadcast(wide), op=ALU.mult,
        )
        inv_std = keep.tile([P, B], F32)
        nc.vector.reciprocal(out=inv_std[:], in_=ln_std[:])
        for b in range(B):
            nc.vector.scalar_tensor_tensor(
                out=result[:, V_COLS * b : V_COLS * (b + 1)], in0=gained[:, b, :],
                scalar=inv_std[:, b : b + 1], in1=bias, op0=ALU.mult, op1=ALU.add,
            )

        result_bank = unit_banks.tile([P, P], F32, tag="logits")
        nc.tensor.transpose(result_bank[:], result[:], identity[:])
        out_rows = keep.tile([P, P], F32)
        nc.vector.tensor_copy(out=out_rows[:], in_=result_bank[:])
        out_view = out.rearrange("b (j p) o -> (b j) (p o)", p=P)
        nc.sync.dma_start(out=out_view[0:STORE_SPLIT, :], in_=out_rows[0:STORE_SPLIT, :])
        nc.scalar.dma_start(
            out=out_view[STORE_SPLIT : B * V_COLS, :], in_=out_rows[STORE_SPLIT : B * V_COLS, :]
        )
